import numpy as np
import ml_dtypes


def mxq(x, axis, fmt="e4m3"):
    dtype, down = {"e4m3": (ml_dtypes.float8_e4m3fn, 7), "e5m2": (ml_dtypes.float8_e5m2, 14)}[fmt]
    v = np.moveaxis(np.asarray(x, np.float32).astype(ml_dtypes.bfloat16).astype(np.float64), axis, -1)
    blocks = v.reshape(v.shape[:-1] + (-1, 32))
    amax = np.abs(blocks).max(-1, keepdims=True)
    byte = np.maximum(np.where(amax > 0, np.frexp(amax)[1] - 1 + 127, 0) - down, 1)
    scale = np.exp2(byte - 127.0)
    codes = (blocks / scale).astype(np.float32).astype(dtype).astype(np.float64)
    return np.moveaxis((codes * scale).reshape(v.shape), -1, axis)


WIDE = False


def mx_kscale(k):
    if not WIDE:
        return np.ones(k)
    levels = np.array([10, -10, 5, -5, 0])
    a = np.random.permutation(np.resize(levels, k // 512 * 4)).reshape(k // 512, 4)
    idx = np.arange(k)
    return np.exp2(a[idx // 512, idx % 128 // 32])


BF16 = ml_dtypes.bfloat16


def bf(x):
    return np.asarray(x, np.float32).astype(BF16)


def f64(x):
    return np.asarray(x).astype(np.float64)


B, NE, D, H = 2, 64, 512, 16
HD = D // H
LN_EPS = 1e-5


def setup_inputs():
    s = mx_kscale(D)
    r = np.exp2(-8.0 * np.random.random_sample((B, NE, 1)))
    return {
        "inp": bf((np.random.standard_normal((B, NE, D)) + 0.5) * r),
        "gamma": bf((1.0 + 0.1 * np.random.standard_normal(D)) * s),
        "beta": bf(0.1 * np.random.standard_normal(D) * s),
        "W_qk": bf(np.random.standard_normal((D, 2 * D)) / np.sqrt(D) / s[:, None]),
        "b_qk": bf(0.1 * np.random.standard_normal(2 * D)),
        "W_v": bf(np.random.standard_normal((D, D)) / np.sqrt(D) / s[:, None]),
        "b_v": bf(0.1 * np.random.standard_normal(D)),
    }


def reference(inp, gamma, beta, W_qk, b_qk, W_v, b_v):
    inp = f64(inp)
    mu = np.mean(inp, axis=-1, keepdims=True)
    var = np.mean(np.square(inp - mu), axis=-1, keepdims=True)
    x = (inp - mu) / np.sqrt(var + LN_EPS) * f64(gamma) + f64(beta)
    xq = mxq(x, 2, "e4m3")
    qk = ((xq @ mxq(f64(W_qk), 0, "e4m3")) + f64(b_qk)).reshape(B, NE, H, HD, 2)
    q = qk[..., 0]
    k = qk[..., 1]
    v = ((xq @ mxq(f64(W_v), 0, "e4m3")) + f64(b_v)).reshape(B, NE, H, HD)
    q = np.transpose(q, (0, 2, 1, 3))
    k = np.transpose(k, (0, 2, 3, 1))
    v = np.transpose(v, (0, 2, 1, 3))
    return (q, k, v)

@@ -1,0 +1,218 @@
+from contextlib import ExitStack
+
+import concourse.mybir as mybir
+from concourse.masks import make_identity
+
+BF16 = mybir.dt.bfloat16
+F32 = mybir.dt.float32
+U32 = mybir.dt.uint32
+U8 = mybir.dt.uint8
+FP8X4 = mybir.dt.float8_e4m3fn_x4
+ALU = mybir.AluOpType
+ACT = mybir.ActivationFunctionType
+
+P = 128
+PACK = 4
+D = P * PACK
+BATCH = 2
+NE = 64
+HD = 32
+HALF = 256
+LN_EPS = 1e-5
+
+FLOPS = 2 * P * D * (3 * D)
+
+
+def tile_relational_s_kernel(tc, inp, gamma, beta, W_qk, b_qk, W_v, b_v, out_0, out_1, out_2):
+    nc = tc.nc
+    with ExitStack() as ctx:
+        keep = ctx.enter_context(tc.tile_pool(name="keep", bufs=1))
+        psum = ctx.enter_context(tc.psum_pool(name="psum", bufs=1))
+        ctx.enter_context(tc.manual_schedule())
+
+        def mx(out, lhsT, lhsT_scale, rhs, rhs_scale):
+            nc.tensor.matmul_mx(
+                out=out,
+                lhsT=lhsT.bitcast(FP8X4),
+                lhsT_scale=lhsT_scale,
+                rhs=rhs.bitcast(FP8X4),
+                rhs_scale=rhs_scale,
+                start=True,
+                stop=True,
+            )
+
+        x_in = keep.tile([P, D], BF16)
+        nc.sync.dma_start(out=x_in[:], in_=inp.flatten_outer_dims())
+        gamma_bf = keep.tile([P, PACK], BF16)
+        nc.scalar.dma_start(out=gamma_bf[:], in_=gamma.rearrange("(p t) -> p t", t=PACK))
+        beta_bf = keep.tile([P, PACK], BF16)
+        nc.scalar.dma_start(out=beta_bf[:], in_=beta.rearrange("(p t) -> p t", t=PACK))
+        raw_v = keep.tile([P, PACK, D], BF16)
+        nc.sync.dma_start(out=raw_v[:], in_=W_v.rearrange("(p t) w -> p t w", t=PACK))
+        raw_qk = []
+        for h in range(2):
+            raw_h = keep.tile([P, PACK, D], BF16, name="raw_qk%d" % h)
+            nc.sync.dma_start(
+                out=raw_h[:], in_=W_qk[:, h * D : (h + 1) * D].rearrange("(p t) w -> p t w", t=PACK)
+            )
+            raw_qk.append(raw_h)
+        bias_k_bf = keep.tile([P, 2, 4], BF16)
+        nc.scalar.dma_start(out=bias_k_bf[:], in_=b_qk.rearrange("(h m r) -> m h r", h=2, r=4))
+        bias_v = keep.tile([P, D], BF16)
+        nc.scalar.dma_start(out=bias_v[:], in_=b_v.partition_broadcast(P))
+        bias_qk = keep.tile([P, 2 * D], BF16)
+        nc.scalar.dma_start(out=bias_qk[:], in_=b_qk.partition_broadcast(P))
+
+        one = keep.tile([P, 1], F32)
+        nc.gpsimd.memset(one[:], 1.0)
+        warm = keep.tile([P, 1], F32)
+        nc.scalar.activation(out=warm[:], in_=one[:], func=ACT.Sqrt)
+        ident = keep.tile([P, P], F32)
+        make_identity(nc, ident[:])
+        gamma_f = keep.tile([P, PACK], F32)
+        nc.gpsimd.tensor_copy(out=gamma_f[:], in_=gamma_bf[:])
+        beta_f = keep.tile([P, PACK], F32)
+        nc.gpsimd.tensor_copy(out=beta_f[:], in_=beta_bf[:])
+        bias_k = keep.tile([P, 2, 2], F32)
+        nc.gpsimd.tensor_copy(
+            out=bias_k[:], in_=bias_k_bf[:].rearrange("m h (c e) -> m e h c", e=2)[:, 1]
+        )
+
+        stats = keep.tile([P, 6], F32)
+        nc.vector.bn_stats(out=stats[:], in_=x_in[:])
+        mean_var = keep.tile([P, 2], F32)
+        nc.vector.bn_aggr(out=mean_var[:], in_=stats[:])
+        var_eps = keep.tile([P, 1], F32)
+        nc.vector.tensor_scalar_add(out=var_eps[:], in0=mean_var[:, 1:2], scalar1=LN_EPS)
+        std = keep.tile([P, 1], F32)
+        nc.scalar.activation(out=std[:], in_=var_eps[:], func=ACT.Sqrt)
+        rstd = keep.tile([P, 1], F32)
+        nc.vector.reciprocal(out=rstd[:], in_=std[:])
+        xhat = keep.tile([P, PACK, P], F32)
+        nc.vector.tensor_scalar(
+            out=xhat[:],
+            in0=x_in[:].rearrange("r (p t) -> r t p", t=PACK),
+            scalar1=mean_var[:, 0:1],
+            scalar2=rstd[:],
+            op0=ALU.subtract,
+            op1=ALU.mult,
+        )
+
+        grouped_v = keep.tile([P, D, PACK], BF16, align_bytes=64)
+        nc.scalar.copy(
+            out=grouped_v[:, HALF:D, :], in_=raw_v[:, :, HALF:D].rearrange("p t w -> p w t")
+        )
+        nc.vector.tensor_copy(
+            out=grouped_v[:, 0:HALF, :], in_=raw_v[:, :, 0:HALF].rearrange("p t w -> p w t")
+        )
+
+        x_planes = keep.tile([P, PACK, P], BF16)
+        for t in range(PACK):
+            xt = psum.tile([P, P], F32, name="xt%d" % t, tag="bank%d" % t)
+            nc.tensor.transpose(xt[:], xhat[:, t, :], ident[:])
+            nc.scalar.activation(
+                out=x_planes[:, t, :],
+                in_=xt[:],
+                func=ACT.Identity,
+                scale=gamma_f[:, t : t + 1],
+                bias=beta_f[:, t : t + 1],
+            )
+
+        grouped_qk = []
+        for h in range(2):
+            grouped = keep.tile([P, 2 * HALF * PACK], BF16, name="grouped_qk%d" % h, align_bytes=64)
+            grouped_qk.append(grouped)
+
+        def regroup_q(h):
+            nc.vector.tensor_copy(
+                out=grouped_qk[h][:, 0 : HALF * PACK].rearrange("p (f t) -> p f t", t=PACK),
+                in_=raw_qk[h][:].rearrange("p t (f e) -> p e f t", e=2)[:, 0],
+            )
+
+        def regroup_k(h):
+            nc.scalar.copy(
+                out=grouped_qk[h][:, HALF * PACK : 2 * HALF * PACK].rearrange(
+                    "p (c m t) -> p c m t", c=2, t=PACK
+                ),
+                in_=raw_qk[h][:].rearrange("p t (m c e) -> p e c m t", c=2, e=2)[:, 1],
+            )
+
+        qk_codes = []
+        qk_scales = []
+        for h in range(2):
+            codes = keep.tile([P, 2 * HALF], U32, name="qk_codes%d" % h, align_bytes=64)
+            scales = keep.tile([P, 2 * HALF], U8, name="qk_scales%d" % h, align_bytes=64)
+            qk_codes.append(codes)
+            qk_scales.append(scales)
+
+        def quantise_qk(h):
+            nc.vector.quantize_mx(
+                out=qk_codes[h][:].bitcast(FP8X4), scales=qk_scales[h][:], in_=grouped_qk[h][:]
+            )
+
+        regroup_q(0)
+        regroup_k(0)
+        regroup_k(1)
+
+        x_grouped = keep.tile([P, P, PACK], BF16, align_bytes=64)
+        nc.vector.tensor_copy(out=x_grouped[:], in_=x_planes[:].rearrange("p t r -> p r t"))
+        v_codes = keep.tile([P, D], U32, align_bytes=64)
+        v_scales = keep.tile([P, D], U8, align_bytes=64)
+        nc.vector.quantize_mx(
+            out=v_codes[:].bitcast(FP8X4),
+            scales=v_scales[:],
+            in_=grouped_v[:].rearrange("p w t -> p (w t)"),
+        )
+        x_codes = keep.tile([P, P], U32, align_bytes=64)
+        x_scales = keep.tile([P, P], U8, align_bytes=64)
+        nc.vector.quantize_mx(
+            out=x_codes[:].bitcast(FP8X4),
+            scales=x_scales[:],
+            in_=x_grouped[:].rearrange("p r t -> p (r t)"),
+        )
+        regroup_q(1)
+        quantise_qk(0)
+
+        acc_v = psum.tile([P, D], F32)
+        mx(acc_v[:], x_codes[:], x_scales[:], v_codes[:], v_scales[:])
+        v_sb = keep.tile([P, D], F32)
+        nc.vector.tensor_tensor(out=v_sb[:], in0=acc_v[:], in1=bias_v[:], op=ALU.add)
+        for b in range(BATCH):
+            nc.sync.dma_start(
+                out=out_2[b].rearrange("h n j -> n h j"),
+                in_=v_sb[b * NE : (b + 1) * NE, :].rearrange("n (h j) -> n h j", j=HD),
+            )
+        quantise_qk(1)
+
+        q_sb = keep.tile([P, D], F32)
+        k_sb = keep.tile([P, BATCH, 2, 2, NE], F32)
+        bias_q = bias_qk[:].rearrange("p (f e) -> p e f", e=2)[:, 0]
+        k_dram = out_1.rearrange("b h j n -> b (h j) n")
+        for h in range(2):
+            codes = qk_codes[h]
+            scales = qk_scales[h]
+            acc_q = psum.tile([P, HALF], F32, name="acc_q%d" % h)
+            mx(acc_q[:], x_codes[:], x_scales[:], codes[:, 0:HALF], scales[:, 0:HALF])
+            cols = slice(h * HALF, (h + 1) * HALF)
+            nc.vector.tensor_tensor(out=q_sb[:, cols], in0=acc_q[:], in1=bias_q[:, cols], op=ALU.add)
+            for c in range(2):
+                acc_k = psum.tile([P, P], F32, name="acc_k%d%d" % (h, c), tag="bank%d" % (2 * h + c))
+                k_cols = slice(HALF + c * P, HALF + (c + 1) * P)
+                mx(acc_k[:], codes[:, k_cols], scales[:, k_cols], x_codes[:], x_scales[:])
+                nc.scalar.activation(
+                    out=k_sb[:, :, h, c, :],
+                    in_=acc_k[:].rearrange("m (b n) -> m b n", b=BATCH),
+                    func=ACT.Identity,
+                    bias=bias_k[:, h, c : c + 1],
+                    scale=1.0,
+                )
+            nc.sync.dma_start(
+                out=k_dram[:, h * HALF : (h + 1) * HALF, :].rearrange("b (m c) n -> m b (c n)", c=2),
+                in_=k_sb[:, :, h, :, :].rearrange("m b c n -> m b (c n)"),
+            )
+            heads = slice(h * HALF // HD, (h + 1) * HALF // HD)
+            for b in range(BATCH):
+                nc.sync.dma_start(
+                    out=out_0[b, heads].rearrange("h n j -> n h j"),
+                    in_=q_sb[b * NE : (b + 1) * NE, cols].rearrange("n (h j) -> n h j", j=HD),
+                )

@@ -56,17 +56,17 @@ def tile_relational_s_kernel(tc, inp, gamma, beta, W_qk, b_qk, W_v, b_v, out_0, 
                 out=raw_h[:], in_=W_qk[:, h * D : (h + 1) * D].rearrange("(p t) w -> p t w", t=PACK)
             )
             raw_qk.append(raw_h)
-        bias_k_bf = keep.tile([P, 2, 4], BF16)
-        nc.scalar.dma_start(out=bias_k_bf[:], in_=b_qk.rearrange("(h m r) -> m h r", h=2, r=4))
-        bias_v = keep.tile([P, D], BF16)
-        nc.scalar.dma_start(out=bias_v[:], in_=b_v.partition_broadcast(P))
-        bias_qk = keep.tile([P, 2 * D], BF16)
-        nc.scalar.dma_start(out=bias_qk[:], in_=b_qk.partition_broadcast(P))
+        b_v_cols = keep.tile([P, PACK], BF16)
+        nc.scalar.dma_start(out=b_v_cols[:], in_=b_v.rearrange("(p c) -> p c", c=PACK))
+        b_qk_cols = keep.tile([P, 2, 4], BF16)
+        nc.scalar.dma_start(out=b_qk_cols[:], in_=b_qk.rearrange("(h m r) -> m h r", h=2, r=4))
 
         one = keep.tile([P, 1], F32)
         nc.gpsimd.memset(one[:], 1.0)
         warm = keep.tile([P, 1], F32)
         nc.scalar.activation(out=warm[:], in_=one[:], func=ACT.Sqrt)
+        ident_bf = keep.tile([P, P], BF16)
+        make_identity(nc, ident_bf[:])
         ident = keep.tile([P, P], F32)
         make_identity(nc, ident[:])
         gamma_f = keep.tile([P, PACK], F32)
@@ -75,8 +75,20 @@ def tile_relational_s_kernel(tc, inp, gamma, beta, W_qk, b_qk, W_v, b_v, out_0, 
         nc.gpsimd.tensor_copy(out=beta_f[:], in_=beta_bf[:])
         bias_k = keep.tile([P, 2, 2], F32)
         nc.gpsimd.tensor_copy(
-            out=bias_k[:], in_=bias_k_bf[:].rearrange("m h (c e) -> m e h c", e=2)[:, 1]
+            out=bias_k[:], in_=b_qk_cols[:].rearrange("m h (c e) -> m e h c", e=2)[:, 1]
         )
+
+        bias_ps = psum.tile([P, 8, P], BF16)
+        for c in range(PACK):
+            nc.tensor.transpose(bias_ps[:, c, :], b_v_cols[:, c : c + 1].to_broadcast([P, P]), ident_bf[:])
+        for h in range(2):
+            for c in range(2):
+                nc.tensor.transpose(
+                    bias_ps[:, 4 + 2 * h + c, :],
+                    b_qk_cols[:, h, 2 * c : 2 * c + 1].to_broadcast([P, P]),
+                    ident_bf[:],
+                )
+        bias_rows = keep.tile([P, 8, P], BF16)
 
         stats = keep.tile([P, 6], F32)
         nc.vector.bn_stats(out=stats[:], in_=x_in[:])
@@ -86,6 +98,7 @@ def tile_relational_s_kernel(tc, inp, gamma, beta, W_qk, b_qk, W_v, b_v, out_0, 
         nc.vector.tensor_scalar_add(out=var_eps[:], in0=mean_var[:, 1:2], scalar1=LN_EPS)
         std = keep.tile([P, 1], F32)
         nc.scalar.activation(out=std[:], in_=var_eps[:], func=ACT.Sqrt)
+        nc.scalar.copy(out=bias_rows[:], in_=bias_ps[:])
         rstd = keep.tile([P, 1], F32)
         nc.vector.reciprocal(out=rstd[:], in_=std[:])
         xhat = keep.tile([P, PACK, P], F32)
@@ -176,7 +189,12 @@ def tile_relational_s_kernel(tc, inp, gamma, beta, W_qk, b_qk, W_v, b_v, out_0, 
         acc_v = psum.tile([P, D], F32)
         mx(acc_v[:], x_codes[:], x_scales[:], v_codes[:], v_scales[:])
         v_sb = keep.tile([P, D], F32)
-        nc.vector.tensor_tensor(out=v_sb[:], in0=acc_v[:], in1=bias_v[:], op=ALU.add)
+        nc.vector.tensor_tensor(
+            out=v_sb[:].rearrange("r (p c) -> r p c", c=PACK),
+            in0=acc_v[:].rearrange("r (p c) -> r p c", c=PACK),
+            in1=bias_rows[:, 0:PACK, :].rearrange("r c p -> r p c"),
+            op=ALU.add,
+        )
         for b in range(BATCH):
             nc.sync.dma_start(
                 out=out_2[b].rearrange("h n j -> n h j"),
@@ -186,7 +204,6 @@ def tile_relational_s_kernel(tc, inp, gamma, beta, W_qk, b_qk, W_v, b_v, out_0, 
 
         q_sb = keep.tile([P, D], F32)
         k_sb = keep.tile([P, BATCH, 2, 2, NE], F32)
-        bias_q = bias_qk[:].rearrange("p (f e) -> p e f", e=2)[:, 0]
         k_dram = out_1.rearrange("b h j n -> b (h j) n")
         for h in range(2):
             codes = qk_codes[h]
@@ -194,7 +211,12 @@ def tile_relational_s_kernel(tc, inp, gamma, beta, W_qk, b_qk, W_v, b_v, out_0, 
             acc_q = psum.tile([P, HALF], F32, name="acc_q%d" % h)
             mx(acc_q[:], x_codes[:], x_scales[:], codes[:, 0:HALF], scales[:, 0:HALF])
             cols = slice(h * HALF, (h + 1) * HALF)
-            nc.vector.tensor_tensor(out=q_sb[:, cols], in0=acc_q[:], in1=bias_q[:, cols], op=ALU.add)
+            nc.vector.tensor_tensor(
+                out=q_sb[:, cols].rearrange("r (m c) -> r m c", c=2),
+                in0=acc_q[:].rearrange("r (m c) -> r m c", c=2),
+                in1=bias_rows[:, 4 + 2 * h : 6 + 2 * h, :].rearrange("r c m -> r m c"),
+                op=ALU.add,
+            )
             for c in range(2):
                 acc_k = psum.tile([P, P], F32, name="acc_k%d%d" % (h, c), tag="bank%d" % (2 * h + c))
                 k_cols = slice(HALF + c * P, HALF + (c + 1) * P)

@@ -18,6 +18,7 @@ BATCH = 2
 NE = 64
 HD = 32
 HALF = 256
+HEADS = HALF // HD
 LN_EPS = 1e-5
 
 FLOPS = 2 * P * D * (3 * D)
@@ -30,7 +31,13 @@ def tile_relational_s_kernel(tc, inp, gamma, beta, W_qk, b_qk, W_v, b_v, out_0, 
         psum = ctx.enter_context(tc.psum_pool(name="psum", bufs=1))
         ctx.enter_context(tc.manual_schedule())
 
-        def mx(out, lhsT, lhsT_scale, rhs, rhs_scale):
+        def row_on_all_partitions(out, column):
+            nc.tensor.transpose(out, column.to_broadcast([P, P]), ident[:])
+
+        def quantise(codes, scales, grouped):
+            nc.vector.quantize_mx(out=codes.bitcast(FP8X4), scales=scales, in_=grouped)
+
+        def multiply(out, lhsT, lhsT_scale, rhs, rhs_scale):
             nc.tensor.matmul_mx(
                 out=out,
                 lhsT=lhsT.bitcast(FP8X4),
@@ -43,10 +50,14 @@ def tile_relational_s_kernel(tc, inp, gamma, beta, W_qk, b_qk, W_v, b_v, out_0, 
 
         x_in = keep.tile([P, D], BF16)
         nc.sync.dma_start(out=x_in[:], in_=inp.flatten_outer_dims())
-        gamma_bf = keep.tile([P, PACK], BF16)
-        nc.scalar.dma_start(out=gamma_bf[:], in_=gamma.rearrange("(p t) -> p t", t=PACK))
-        beta_bf = keep.tile([P, PACK], BF16)
-        nc.scalar.dma_start(out=beta_bf[:], in_=beta.rearrange("(p t) -> p t", t=PACK))
+        gamma_cols = keep.tile([P, PACK], BF16)
+        nc.scalar.dma_start(out=gamma_cols[:], in_=gamma.rearrange("(p t) -> p t", t=PACK))
+        beta_cols = keep.tile([P, PACK], BF16)
+        nc.scalar.dma_start(out=beta_cols[:], in_=beta.rearrange("(p t) -> p t", t=PACK))
+        b_v_cols = keep.tile([P, PACK], BF16)
+        nc.scalar.dma_start(out=b_v_cols[:], in_=b_v.rearrange("(p t) -> p t", t=PACK))
+        b_qk_cols = keep.tile([P, 2, 4], BF16)
+        nc.scalar.dma_start(out=b_qk_cols[:], in_=b_qk.rearrange("(h m r) -> m h r", h=2, r=4))
         raw_v = keep.tile([P, PACK, D], BF16)
         nc.sync.dma_start(out=raw_v[:], in_=W_v.rearrange("(p t) w -> p t w", t=PACK))
         raw_qk = []
@@ -56,173 +67,148 @@ def tile_relational_s_kernel(tc, inp, gamma, beta, W_qk, b_qk, W_v, b_v, out_0, 
                 out=raw_h[:], in_=W_qk[:, h * D : (h + 1) * D].rearrange("(p t) w -> p t w", t=PACK)
             )
             raw_qk.append(raw_h)
-        b_v_cols = keep.tile([P, PACK], BF16)
-        nc.scalar.dma_start(out=b_v_cols[:], in_=b_v.rearrange("(p c) -> p c", c=PACK))
-        b_qk_cols = keep.tile([P, 2, 4], BF16)
-        nc.scalar.dma_start(out=b_qk_cols[:], in_=b_qk.rearrange("(h m r) -> m h r", h=2, r=4))
 
-        one = keep.tile([P, 1], F32)
-        nc.gpsimd.memset(one[:], 1.0)
-        warm = keep.tile([P, 1], F32)
-        nc.scalar.activation(out=warm[:], in_=one[:], func=ACT.Sqrt)
-        ident_bf = keep.tile([P, P], BF16)
-        make_identity(nc, ident_bf[:])
-        ident = keep.tile([P, P], F32)
+        ident = keep.tile([P, P], BF16)
         make_identity(nc, ident[:])
-        gamma_f = keep.tile([P, PACK], F32)
-        nc.gpsimd.tensor_copy(out=gamma_f[:], in_=gamma_bf[:])
-        beta_f = keep.tile([P, PACK], F32)
-        nc.gpsimd.tensor_copy(out=beta_f[:], in_=beta_bf[:])
+        zero = keep.tile([P, 1], F32)
+        nc.gpsimd.memset(zero[:], 0.0)
+        eps = keep.tile([P, 1], F32)
+        nc.vector.tensor_scalar_add(out=eps[:], in0=zero[:], scalar1=LN_EPS)
+        warm = keep.tile([P, 1], F32)
+        nc.scalar.activation(out=warm[:], in_=eps[:], func=ACT.Sqrt)
         bias_k = keep.tile([P, 2, 2], F32)
         nc.gpsimd.tensor_copy(
             out=bias_k[:], in_=b_qk_cols[:].rearrange("m h (c e) -> m e h c", e=2)[:, 1]
         )
 
-        bias_ps = psum.tile([P, 8, P], BF16)
-        for c in range(PACK):
-            nc.tensor.transpose(bias_ps[:, c, :], b_v_cols[:, c : c + 1].to_broadcast([P, P]), ident_bf[:])
+        gamma_rows = psum.tile([P, PACK, P], BF16, tag="bank0")
+        for t in range(PACK):
+            row_on_all_partitions(gamma_rows[:, t, :], gamma_cols[:, t : t + 1])
+        beta_rows = psum.tile([P, PACK, P], BF16, tag="bank1")
+        for t in range(PACK):
+            row_on_all_partitions(beta_rows[:, t, :], beta_cols[:, t : t + 1])
+        bias_ps = psum.tile([P, 2 * PACK, P], BF16, tag="bank2")
+        for t in range(PACK):
+            row_on_all_partitions(bias_ps[:, t, :], b_v_cols[:, t : t + 1])
         for h in range(2):
             for c in range(2):
-                nc.tensor.transpose(
-                    bias_ps[:, 4 + 2 * h + c, :],
-                    b_qk_cols[:, h, 2 * c : 2 * c + 1].to_broadcast([P, P]),
-                    ident_bf[:],
-                )
-        bias_rows = keep.tile([P, 8, P], BF16)
+                row_on_all_partitions(bias_ps[:, PACK + 2 * h + c, :], b_qk_cols[:, h, 2 * c : 2 * c + 1])
 
         stats = keep.tile([P, 6], F32)
         nc.vector.bn_stats(out=stats[:], in_=x_in[:])
         mean_var = keep.tile([P, 2], F32)
         nc.vector.bn_aggr(out=mean_var[:], in_=stats[:])
-        var_eps = keep.tile([P, 1], F32)
-        nc.vector.tensor_scalar_add(out=var_eps[:], in0=mean_var[:, 1:2], scalar1=LN_EPS)
         std = keep.tile([P, 1], F32)
-        nc.scalar.activation(out=std[:], in_=var_eps[:], func=ACT.Sqrt)
-        nc.scalar.copy(out=bias_rows[:], in_=bias_ps[:])
-        rstd = keep.tile([P, 1], F32)
-        nc.vector.reciprocal(out=rstd[:], in_=std[:])
-        xhat = keep.tile([P, PACK, P], F32)
-        nc.vector.tensor_scalar(
-            out=xhat[:],
+        nc.scalar.activation(out=std[:], in_=mean_var[:, 1:2], func=ACT.Sqrt, bias=eps[:], scale=1.0)
+        centred = keep.tile([P, PACK, P], F32)
+        nc.vector.scalar_tensor_tensor(
+            out=centred[:],
             in0=x_in[:].rearrange("r (p t) -> r t p", t=PACK),
-            scalar1=mean_var[:, 0:1],
-            scalar2=rstd[:],
+            scalar=mean_var[:, 0:1],
+            in1=gamma_rows[:],
             op0=ALU.subtract,
             op1=ALU.mult,
         )
+        rstd = keep.tile([P, 1], F32)
+        nc.vector.reciprocal(out=rstd[:], in_=std[:])
+        x_bf = keep.tile([P, PACK, P], BF16)
+        nc.vector.scalar_tensor_tensor(
+            out=x_bf[:], in0=centred[:], scalar=rstd[:], in1=beta_rows[:], op0=ALU.mult, op1=ALU.add
+        )
+
+        x_t = psum.tile([P, PACK, P], BF16, tag="bank3")
+        for t in range(PACK):
+            nc.tensor.transpose(x_t[:, t, :], x_bf[:, t, :], ident[:])
+        x_grouped = keep.tile([P, P, PACK], BF16, align_bytes=64)
+        x_codes = keep.tile([P, P], U32, align_bytes=64)
+        x_scales = keep.tile([P, P], U8, align_bytes=64)
 
         grouped_v = keep.tile([P, D, PACK], BF16, align_bytes=64)
-        nc.scalar.copy(
-            out=grouped_v[:, HALF:D, :], in_=raw_v[:, :, HALF:D].rearrange("p t w -> p w t")
-        )
-        nc.vector.tensor_copy(
-            out=grouped_v[:, 0:HALF, :], in_=raw_v[:, :, 0:HALF].rearrange("p t w -> p w t")
-        )
-
-        x_planes = keep.tile([P, PACK, P], BF16)
-        for t in range(PACK):
-            xt = psum.tile([P, P], F32, name="xt%d" % t, tag="bank%d" % t)
-            nc.tensor.transpose(xt[:], xhat[:, t, :], ident[:])
-            nc.scalar.activation(
-                out=x_planes[:, t, :],
-                in_=xt[:],
-                func=ACT.Identity,
-                scale=gamma_f[:, t : t + 1],
-                bias=beta_f[:, t : t + 1],
-            )
-
-        grouped_qk = []
+        v_codes = keep.tile([P, D], U32, align_bytes=64)
+        v_scales = keep.tile([P, D], U8, align_bytes=64)
+        grouped_q = []
+        grouped_k = []
+        q_codes = []
+        q_scales = []
+        k_codes = []
+        k_scales = []
         for h in range(2):
-            grouped = keep.tile([P, 2 * HALF * PACK], BF16, name="grouped_qk%d" % h, align_bytes=64)
-            grouped_qk.append(grouped)
+            grouped_q.append(keep.tile([P, HALF, PACK], BF16, name="grouped_q%d" % h, align_bytes=64))
+            grouped_k.append(keep.tile([P, 2, P, PACK], BF16, name="grouped_k%d" % h, align_bytes=64))
+            q_codes.append(keep.tile([P, HALF], U32, name="q_codes%d" % h, align_bytes=64))
+            q_scales.append(keep.tile([P, HALF], U8, name="q_scales%d" % h, align_bytes=64))
+            k_codes.append(keep.tile([P, HALF], U32, name="k_codes%d" % h, align_bytes=64))
+            k_scales.append(keep.tile([P, HALF], U8, name="k_scales%d" % h, align_bytes=64))
 
         def regroup_q(h):
             nc.vector.tensor_copy(
-                out=grouped_qk[h][:, 0 : HALF * PACK].rearrange("p (f t) -> p f t", t=PACK),
-                in_=raw_qk[h][:].rearrange("p t (f e) -> p e f t", e=2)[:, 0],
+                out=grouped_q[h][:], in_=raw_qk[h][:].rearrange("p t (f e) -> p e f t", e=2)[:, 0]
             )
 
-        def regroup_k(h):
+        def regroup_k(h, c):
             nc.scalar.copy(
-                out=grouped_qk[h][:, HALF * PACK : 2 * HALF * PACK].rearrange(
-                    "p (c m t) -> p c m t", c=2, t=PACK
-                ),
-                in_=raw_qk[h][:].rearrange("p t (m c e) -> p e c m t", c=2, e=2)[:, 1],
+                out=grouped_k[h][:, c],
+                in_=raw_qk[h][:].rearrange("p t (m c e) -> p c e m t", c=2, e=2)[:, c, 1],
             )
 
-        qk_codes = []
-        qk_scales = []
-        for h in range(2):
-            codes = keep.tile([P, 2 * HALF], U32, name="qk_codes%d" % h, align_bytes=64)
-            scales = keep.tile([P, 2 * HALF], U8, name="qk_scales%d" % h, align_bytes=64)
-            qk_codes.append(codes)
-            qk_scales.append(scales)
+        bias_rows = keep.tile([P, 2 * PACK, P], BF16)
 
-        def quantise_qk(h):
-            nc.vector.quantize_mx(
-                out=qk_codes[h][:].bitcast(FP8X4), scales=qk_scales[h][:], in_=grouped_qk[h][:]
-            )
+        nc.scalar.copy(out=grouped_v[:, HALF:D, :], in_=raw_v[:, :, HALF:D].rearrange("p t w -> p w t"))
+        regroup_k(0, 0)
+        nc.scalar.copy(out=x_grouped[:], in_=x_t[:].rearrange("p t r -> p r t"))
+        nc.scalar.copy(out=bias_rows[:], in_=bias_ps[:])
+        regroup_k(0, 1)
+        regroup_k(1, 0)
+        regroup_k(1, 1)
 
+        nc.vector.tensor_copy(out=grouped_v[:, 0:HALF, :], in_=raw_v[:, :, 0:HALF].rearrange("p t w -> p w t"))
+        quantise(v_codes[:], v_scales[:], grouped_v[:].rearrange("p w t -> p (w t)"))
         regroup_q(0)
-        regroup_k(0)
-        regroup_k(1)
-
-        x_grouped = keep.tile([P, P, PACK], BF16, align_bytes=64)
-        nc.vector.tensor_copy(out=x_grouped[:], in_=x_planes[:].rearrange("p t r -> p r t"))
-        v_codes = keep.tile([P, D], U32, align_bytes=64)
-        v_scales = keep.tile([P, D], U8, align_bytes=64)
-        nc.vector.quantize_mx(
-            out=v_codes[:].bitcast(FP8X4),
-            scales=v_scales[:],
-            in_=grouped_v[:].rearrange("p w t -> p (w t)"),
-        )
-        x_codes = keep.tile([P, P], U32, align_bytes=64)
-        x_scales = keep.tile([P, P], U8, align_bytes=64)
-        nc.vector.quantize_mx(
-            out=x_codes[:].bitcast(FP8X4),
-            scales=x_scales[:],
-            in_=x_grouped[:].rearrange("p r t -> p (r t)"),
-        )
+        quantise(x_codes[:], x_scales[:], x_grouped[:].rearrange("p r t -> p (r t)"))
+        quantise(q_codes[0][:], q_scales[0][:], grouped_q[0][:].rearrange("p f t -> p (f t)"))
         regroup_q(1)
-        quantise_qk(0)
 
-        acc_v = psum.tile([P, D], F32)
-        mx(acc_v[:], x_codes[:], x_scales[:], v_codes[:], v_scales[:])
-        v_sb = keep.tile([P, D], F32)
-        nc.vector.tensor_tensor(
-            out=v_sb[:].rearrange("r (p c) -> r p c", c=PACK),
-            in0=acc_v[:].rearrange("r (p c) -> r p c", c=PACK),
-            in1=bias_rows[:, 0:PACK, :].rearrange("r c p -> r p c"),
-            op=ALU.add,
-        )
-        for b in range(BATCH):
-            nc.sync.dma_start(
-                out=out_2[b].rearrange("h n j -> n h j"),
-                in_=v_sb[b * NE : (b + 1) * NE, :].rearrange("n (h j) -> n h j", j=HD),
-            )
-        quantise_qk(1)
-
-        q_sb = keep.tile([P, D], F32)
-        k_sb = keep.tile([P, BATCH, 2, 2, NE], F32)
-        k_dram = out_1.rearrange("b h j n -> b (h j) n")
-        for h in range(2):
-            codes = qk_codes[h]
-            scales = qk_scales[h]
-            acc_q = psum.tile([P, HALF], F32, name="acc_q%d" % h)
-            mx(acc_q[:], x_codes[:], x_scales[:], codes[:, 0:HALF], scales[:, 0:HALF])
-            cols = slice(h * HALF, (h + 1) * HALF)
+        def project(name, h, codes, scales, bias, out_dram):
+            acc = psum.tile([P, HALF], F32, name="acc_%s%d" % (name, h))
+            multiply(acc[:], x_codes[:], x_scales[:], codes, scales)
+            width = bias.shape[2]
+            result = keep.tile([P, HALF], F32, name="%s_sb%d" % (name, h))
             nc.vector.tensor_tensor(
-                out=q_sb[:, cols].rearrange("r (m c) -> r m c", c=2),
-                in0=acc_q[:].rearrange("r (m c) -> r m c", c=2),
-                in1=bias_rows[:, 4 + 2 * h : 6 + 2 * h, :].rearrange("r c m -> r m c"),
+                out=result[:].rearrange("r (m c) -> r m c", c=width),
+                in0=acc[:].rearrange("r (m c) -> r m c", c=width),
+                in1=bias,
                 op=ALU.add,
             )
+            for b in range(BATCH):
+                nc.sync.dma_start(
+                    out=out_dram[b, h * HEADS : (h + 1) * HEADS].rearrange("h n j -> n h j"),
+                    in_=result[b * NE : (b + 1) * NE, :].rearrange("n (h j) -> n h j", j=HD),
+                )
+
+        def bias_of_v(h):
+            return bias_rows[:, 0:PACK, h * NE : (h + 1) * NE].rearrange("r t p -> r p t")
+
+        def bias_of_q(h):
+            return bias_rows[:, PACK + 2 * h : PACK + 2 * h + 2, :].rearrange("r c m -> r m c")
+
+        for h in range(2):
+            cols = slice(h * HALF, (h + 1) * HALF)
+            project("v", h, v_codes[:, cols], v_scales[:, cols], bias_of_v(h), out_2)
+        project("q", 0, q_codes[0][:], q_scales[0][:], bias_of_q(0), out_0)
+        quantise(q_codes[1][:], q_scales[1][:], grouped_q[1][:].rearrange("p f t -> p (f t)"))
+        quantise(k_codes[0][:], k_scales[0][:], grouped_k[0][:].rearrange("p c m t -> p (c m t)"))
+        project("q", 1, q_codes[1][:], q_scales[1][:], bias_of_q(1), out_0)
+        quantise(k_codes[1][:], k_scales[1][:], grouped_k[1][:].rearrange("p c m t -> p (c m t)"))
+
+        k_dram = out_1.rearrange("b h j n -> b (h j) n")
+        for h in range(2):
+            k_sb = keep.tile([P, BATCH, 2, NE], F32, name="k_sb%d" % h)
             for c in range(2):
                 acc_k = psum.tile([P, P], F32, name="acc_k%d%d" % (h, c), tag="bank%d" % (2 * h + c))
-                k_cols = slice(HALF + c * P, HALF + (c + 1) * P)
-                mx(acc_k[:], codes[:, k_cols], scales[:, k_cols], x_codes[:], x_scales[:])
+                m_cols = slice(c * P, (c + 1) * P)
+                multiply(acc_k[:], k_codes[h][:, m_cols], k_scales[h][:, m_cols], x_codes[:], x_scales[:])
                 nc.scalar.activation(
-                    out=k_sb[:, :, h, c, :],
+                    out=k_sb[:, :, c, :],
                     in_=acc_k[:].rearrange("m (b n) -> m b n", b=BATCH),
                     func=ACT.Identity,
                     bias=bias_k[:, h, c : c + 1],
@@ -230,11 +216,5 @@ def tile_relational_s_kernel(tc, inp, gamma, beta, W_qk, b_qk, W_v, b_v, out_0, 
                 )
             nc.sync.dma_start(
                 out=k_dram[:, h * HALF : (h + 1) * HALF, :].rearrange("b (m c) n -> m b (c n)", c=2),
-                in_=k_sb[:, :, h, :, :].rearrange("m b c n -> m b (c n)"),
+                in_=k_sb[:].rearrange("m b c n -> m b (c n)"),
             )
-            heads = slice(h * HALF // HD, (h + 1) * HALF // HD)
-            for b in range(BATCH):
-                nc.sync.dma_start(
-                    out=out_0[b, heads].rearrange("h n j -> n h j"),
-                    in_=q_sb[b * NE : (b + 1) * NE, cols].rearrange("n (h j) -> n h j", j=HD),
-                )

@@ -49,7 +49,8 @@ def tile_relational_s_kernel(tc, inp, gamma, beta, W_qk, b_qk, W_v, b_v, out_0, 
             )
 
         x_in = keep.tile([P, D], BF16)
-        nc.sync.dma_start(out=x_in[:], in_=inp.flatten_outer_dims())
+        nc.sync.dma_start(out=x_in[0:P:BATCH, :], in_=inp[0])
+        nc.scalar.dma_start(out=x_in[1:P:BATCH, :], in_=inp[1])
         gamma_cols = keep.tile([P, PACK], BF16)
         nc.scalar.dma_start(out=gamma_cols[:], in_=gamma.rearrange("(p t) -> p t", t=PACK))
         beta_cols = keep.tile([P, PACK], BF16)
@@ -182,7 +183,7 @@ def tile_relational_s_kernel(tc, inp, gamma, beta, W_qk, b_qk, W_v, b_v, out_0, 
             for b in range(BATCH):
                 nc.sync.dma_start(
                     out=out_dram[b, h * HEADS : (h + 1) * HEADS].rearrange("h n j -> n h j"),
-                    in_=result[b * NE : (b + 1) * NE, :].rearrange("n (h j) -> n h j", j=HD),
+                    in_=result[b:P:BATCH, :].rearrange("n (h j) -> n h j", j=HD),
                 )
 
         def bias_of_v(h):
@@ -209,7 +210,7 @@ def tile_relational_s_kernel(tc, inp, gamma, beta, W_qk, b_qk, W_v, b_v, out_0, 
                 multiply(acc_k[:], k_codes[h][:, m_cols], k_scales[h][:, m_cols], x_codes[:], x_scales[:])
                 nc.scalar.activation(
                     out=k_sb[:, :, c, :],
-                    in_=acc_k[:].rearrange("m (b n) -> m b n", b=BATCH),
+                    in_=acc_k[:].rearrange("m (n b) -> m b n", b=BATCH),
                     func=ACT.Identity,
                     bias=bias_k[:, h, c : c + 1],
                     scale=1.0,

@@ -19,6 +19,7 @@ NE = 64
 HD = 32
 HALF = 256
 HEADS = HALF // HD
+RUN = 4
 LN_EPS = 1e-5
 
 FLOPS = 2 * P * D * (3 * D)
@@ -49,8 +50,7 @@ def tile_relational_s_kernel(tc, inp, gamma, beta, W_qk, b_qk, W_v, b_v, out_0, 
             )
 
         x_in = keep.tile([P, D], BF16)
-        nc.sync.dma_start(out=x_in[0:P:BATCH, :], in_=inp[0])
-        nc.scalar.dma_start(out=x_in[1:P:BATCH, :], in_=inp[1])
+        nc.sync.dma_start(out=x_in[:], in_=inp.flatten_outer_dims())
         gamma_cols = keep.tile([P, PACK], BF16)
         nc.scalar.dma_start(out=gamma_cols[:], in_=gamma.rearrange("(p t) -> p t", t=PACK))
         beta_cols = keep.tile([P, PACK], BF16)
@@ -113,13 +113,19 @@ def tile_relational_s_kernel(tc, inp, gamma, beta, W_qk, b_qk, W_v, b_v, out_0, 
         rstd = keep.tile([P, 1], F32)
         nc.vector.reciprocal(out=rstd[:], in_=std[:])
         x_bf = keep.tile([P, PACK, P], BF16)
-        nc.vector.scalar_tensor_tensor(
-            out=x_bf[:], in0=centred[:], scalar=rstd[:], in1=beta_rows[:], op0=ALU.mult, op1=ALU.add
-        )
-
         x_t = psum.tile([P, PACK, P], BF16, tag="bank3")
-        for t in range(PACK):
-            nc.tensor.transpose(x_t[:, t, :], x_bf[:, t, :], ident[:])
+        for first in range(0, PACK, 2):
+            pair = slice(first, first + 2)
+            nc.vector.scalar_tensor_tensor(
+                out=x_bf[:, pair, :],
+                in0=centred[:, pair, :],
+                scalar=rstd[:],
+                in1=beta_rows[:, pair, :],
+                op0=ALU.mult,
+                op1=ALU.add,
+            )
+            for t in range(first, first + 2):
+                nc.tensor.transpose(x_t[:, t, :], x_bf[:, t, :], ident[:])
         x_grouped = keep.tile([P, P, PACK], BF16, align_bytes=64)
         x_codes = keep.tile([P, P], U32, align_bytes=64)
         x_scales = keep.tile([P, P], U8, align_bytes=64)
@@ -141,20 +147,27 @@ def tile_relational_s_kernel(tc, inp, gamma, beta, W_qk, b_qk, W_v, b_v, out_0, 
             k_codes.append(keep.tile([P, HALF], U32, name="k_codes%d" % h, align_bytes=64))
             k_scales.append(keep.tile([P, HALF], U8, name="k_scales%d" % h, align_bytes=64))
 
+        def as_runs(grouped):
+            return grouped.rearrange("p (a i) t -> p a t i", i=RUN)
+
+        def regroup_v(copy, cols):
+            copy(out=as_runs(grouped_v[:, cols, :]), in_=raw_v[:, :, cols].rearrange("p t (a i) -> p a t i", i=RUN))
+
         def regroup_q(h):
             nc.vector.tensor_copy(
-                out=grouped_q[h][:], in_=raw_qk[h][:].rearrange("p t (f e) -> p e f t", e=2)[:, 0]
+                out=as_runs(grouped_q[h][:]),
+                in_=raw_qk[h][:].rearrange("p t (a i e) -> p e a t i", i=RUN, e=2)[:, 0],
             )
 
         def regroup_k(h, c):
             nc.scalar.copy(
-                out=grouped_k[h][:, c],
-                in_=raw_qk[h][:].rearrange("p t (m c e) -> p c e m t", c=2, e=2)[:, c, 1],
+                out=as_runs(grouped_k[h][:, c]),
+                in_=raw_qk[h][:].rearrange("p t (a i c e) -> p c e a t i", i=RUN, c=2, e=2)[:, c, 1],
             )
 
         bias_rows = keep.tile([P, 2 * PACK, P], BF16)
 
-        nc.scalar.copy(out=grouped_v[:, HALF:D, :], in_=raw_v[:, :, HALF:D].rearrange("p t w -> p w t"))
+        regroup_v(nc.scalar.copy, slice(HALF, D))
         regroup_k(0, 0)
         nc.scalar.copy(out=x_grouped[:], in_=x_t[:].rearrange("p t r -> p r t"))
         nc.scalar.copy(out=bias_rows[:], in_=bias_ps[:])
@@ -162,11 +175,10 @@ def tile_relational_s_kernel(tc, inp, gamma, beta, W_qk, b_qk, W_v, b_v, out_0, 
         regroup_k(1, 0)
         regroup_k(1, 1)
 
-        nc.vector.tensor_copy(out=grouped_v[:, 0:HALF, :], in_=raw_v[:, :, 0:HALF].rearrange("p t w -> p w t"))
+        regroup_v(nc.vector.tensor_copy, slice(0, HALF))
         quantise(v_codes[:], v_scales[:], grouped_v[:].rearrange("p w t -> p (w t)"))
-        regroup_q(0)
         quantise(x_codes[:], x_scales[:], x_grouped[:].rearrange("p r t -> p (r t)"))
-        quantise(q_codes[0][:], q_scales[0][:], grouped_q[0][:].rearrange("p f t -> p (f t)"))
+        regroup_q(0)
         regroup_q(1)
 
         def project(name, h, codes, scales, bias, out_dram):
@@ -183,7 +195,7 @@ def tile_relational_s_kernel(tc, inp, gamma, beta, W_qk, b_qk, W_v, b_v, out_0, 
             for b in range(BATCH):
                 nc.sync.dma_start(
                     out=out_dram[b, h * HEADS : (h + 1) * HEADS].rearrange("h n j -> n h j"),
-                    in_=result[b:P:BATCH, :].rearrange("n (h j) -> n h j", j=HD),
+                    in_=result[b * NE : (b + 1) * NE, :].rearrange("n (h j) -> n h j", j=HD),
                 )
 
         def bias_of_v(h):
@@ -195,11 +207,10 @@ def tile_relational_s_kernel(tc, inp, gamma, beta, W_qk, b_qk, W_v, b_v, out_0, 
         for h in range(2):
             cols = slice(h * HALF, (h + 1) * HALF)
             project("v", h, v_codes[:, cols], v_scales[:, cols], bias_of_v(h), out_2)
-        project("q", 0, q_codes[0][:], q_scales[0][:], bias_of_q(0), out_0)
-        quantise(q_codes[1][:], q_scales[1][:], grouped_q[1][:].rearrange("p f t -> p (f t)"))
-        quantise(k_codes[0][:], k_scales[0][:], grouped_k[0][:].rearrange("p c m t -> p (c m t)"))
-        project("q", 1, q_codes[1][:], q_scales[1][:], bias_of_q(1), out_0)
-        quantise(k_codes[1][:], k_scales[1][:], grouped_k[1][:].rearrange("p c m t -> p (c m t)"))
+            quantise(q_codes[h][:], q_scales[h][:], grouped_q[h][:].rearrange("p f t -> p (f t)"))
+        for h in range(2):
+            project("q", h, q_codes[h][:], q_scales[h][:], bias_of_q(h), out_0)
+            quantise(k_codes[h][:], k_scales[h][:], grouped_k[h][:].rearrange("p c m t -> p (c m t)"))
 
         k_dram = out_1.rearrange("b h j n -> b (h j) n")
         for h in range(2):
@@ -210,7 +221,7 @@ def tile_relational_s_kernel(tc, inp, gamma, beta, W_qk, b_qk, W_v, b_v, out_0, 
                 multiply(acc_k[:], k_codes[h][:, m_cols], k_scales[h][:, m_cols], x_codes[:], x_scales[:])
                 nc.scalar.activation(
                     out=k_sb[:, :, c, :],
-                    in_=acc_k[:].rearrange("m (n b) -> m b n", b=BATCH),
+                    in_=acc_k[:].rearrange("m (b n) -> m b n", b=BATCH),
                     func=ACT.Identity,
                     bias=bias_k[:, h, c : c + 1],
                     scale=1.0,

@@ -56,11 +56,16 @@ def tile_relational_s_kernel(tc, inp, gamma, beta, W_qk, b_qk, W_v, b_v, out_0, 
         beta_cols = keep.tile([P, PACK], BF16)
         nc.scalar.dma_start(out=beta_cols[:], in_=beta.rearrange("(p t) -> p t", t=PACK))
         b_v_cols = keep.tile([P, PACK], BF16)
-        nc.scalar.dma_start(out=b_v_cols[:], in_=b_v.rearrange("(p t) -> p t", t=PACK))
+        nc.sync.dma_start(out=b_v_cols[:], in_=b_v.rearrange("(p t) -> p t", t=PACK))
         b_qk_cols = keep.tile([P, 2, 4], BF16)
-        nc.scalar.dma_start(out=b_qk_cols[:], in_=b_qk.rearrange("(h m r) -> m h r", h=2, r=4))
-        raw_v = keep.tile([P, PACK, D], BF16)
-        nc.sync.dma_start(out=raw_v[:], in_=W_v.rearrange("(p t) w -> p t w", t=PACK))
+        nc.sync.dma_start(out=b_qk_cols[:], in_=b_qk.rearrange("(h m r) -> m h r", h=2, r=4))
+        raw_v = []
+        for h in range(2):
+            raw_h = keep.tile([P, PACK, HALF], BF16, name="raw_v%d" % h)
+            nc.sync.dma_start(
+                out=raw_h[:], in_=W_v[:, h * HALF : (h + 1) * HALF].rearrange("(p t) w -> p t w", t=PACK)
+            )
+            raw_v.append(raw_h)
         raw_qk = []
         for h in range(2):
             raw_h = keep.tile([P, PACK, D], BF16, name="raw_qk%d" % h)
@@ -88,12 +93,6 @@ def tile_relational_s_kernel(tc, inp, gamma, beta, W_qk, b_qk, W_v, b_v, out_0, 
         beta_rows = psum.tile([P, PACK, P], BF16, tag="bank1")
         for t in range(PACK):
             row_on_all_partitions(beta_rows[:, t, :], beta_cols[:, t : t + 1])
-        bias_ps = psum.tile([P, 2 * PACK, P], BF16, tag="bank2")
-        for t in range(PACK):
-            row_on_all_partitions(bias_ps[:, t, :], b_v_cols[:, t : t + 1])
-        for h in range(2):
-            for c in range(2):
-                row_on_all_partitions(bias_ps[:, PACK + 2 * h + c, :], b_qk_cols[:, h, 2 * c : 2 * c + 1])
 
         stats = keep.tile([P, 6], F32)
         nc.vector.bn_stats(out=stats[:], in_=x_in[:])
@@ -126,69 +125,71 @@ def tile_relational_s_kernel(tc, inp, gamma, beta, W_qk, b_qk, W_v, b_v, out_0, 
             )
             for t in range(first, first + 2):
                 nc.tensor.transpose(x_t[:, t, :], x_bf[:, t, :], ident[:])
+        bias_ps = psum.tile([P, 2 * PACK, P], BF16, tag="bank2")
+        for t in range(PACK):
+            row_on_all_partitions(bias_ps[:, t, :], b_v_cols[:, t : t + 1])
+        for h in range(2):
+            for c in range(2):
+                row_on_all_partitions(bias_ps[:, PACK + 2 * h + c, :], b_qk_cols[:, h, 2 * c : 2 * c + 1])
+
         x_grouped = keep.tile([P, P, PACK], BF16, align_bytes=64)
         x_codes = keep.tile([P, P], U32, align_bytes=64)
         x_scales = keep.tile([P, P], U8, align_bytes=64)
 
-        grouped_v = keep.tile([P, D, PACK], BF16, align_bytes=64)
-        v_codes = keep.tile([P, D], U32, align_bytes=64)
-        v_scales = keep.tile([P, D], U8, align_bytes=64)
-        grouped_q = []
-        grouped_k = []
-        q_codes = []
-        q_scales = []
-        k_codes = []
-        k_scales = []
-        for h in range(2):
-            grouped_q.append(keep.tile([P, HALF, PACK], BF16, name="grouped_q%d" % h, align_bytes=64))
-            grouped_k.append(keep.tile([P, 2, P, PACK], BF16, name="grouped_k%d" % h, align_bytes=64))
-            q_codes.append(keep.tile([P, HALF], U32, name="q_codes%d" % h, align_bytes=64))
-            q_scales.append(keep.tile([P, HALF], U8, name="q_scales%d" % h, align_bytes=64))
-            k_codes.append(keep.tile([P, HALF], U32, name="k_codes%d" % h, align_bytes=64))
-            k_scales.append(keep.tile([P, HALF], U8, name="k_scales%d" % h, align_bytes=64))
+        grouped = {}
+        codes = {}
+        scales = {}
+        for name in ("v", "q", "k"):
+            for h in range(2):
+                grouped[name, h] = keep.tile([P, HALF, PACK], BF16, name="grouped_%s%d" % (name, h), align_bytes=64)
+                codes[name, h] = keep.tile([P, HALF], U32, name="codes_%s%d" % (name, h), align_bytes=64)
+                scales[name, h] = keep.tile([P, HALF], U8, name="scales_%s%d" % (name, h), align_bytes=64)
 
-        def as_runs(grouped):
-            return grouped.rearrange("p (a i) t -> p a t i", i=RUN)
+        def as_runs(part):
+            return part.rearrange("p (a i) t -> p a t i", i=RUN)
 
-        def regroup_v(copy, cols):
-            copy(out=as_runs(grouped_v[:, cols, :]), in_=raw_v[:, :, cols].rearrange("p t (a i) -> p a t i", i=RUN))
+        def regroup_v(copy, h):
+            copy(out=as_runs(grouped["v", h][:]), in_=raw_v[h][:].rearrange("p t (a i) -> p a t i", i=RUN))
 
-        def regroup_q(h):
-            nc.vector.tensor_copy(
-                out=as_runs(grouped_q[h][:]),
+        def regroup_q(copy, h):
+            copy(
+                out=as_runs(grouped["q", h][:]),
                 in_=raw_qk[h][:].rearrange("p t (a i e) -> p e a t i", i=RUN, e=2)[:, 0],
             )
 
-        def regroup_k(h, c):
-            nc.scalar.copy(
-                out=as_runs(grouped_k[h][:, c]),
+        def regroup_k(copy, h, c):
+            copy(
+                out=as_runs(grouped["k", h][:, c * P : (c + 1) * P, :]),
                 in_=raw_qk[h][:].rearrange("p t (a i c e) -> p c e a t i", i=RUN, c=2, e=2)[:, c, 1],
             )
 
-        bias_rows = keep.tile([P, 2 * PACK, P], BF16)
+        def quantise_w(name, h):
+            quantise(codes[name, h][:], scales[name, h][:], grouped[name, h][:].rearrange("p f t -> p (f t)"))
 
-        regroup_v(nc.scalar.copy, slice(HALF, D))
-        regroup_k(0, 0)
+        bias_v_rows = keep.tile([P, PACK, P], BF16)
+        bias_q_rows = keep.tile([P, PACK, P], BF16)
+
+        regroup_v(nc.scalar.copy, 0)
         nc.scalar.copy(out=x_grouped[:], in_=x_t[:].rearrange("p t r -> p r t"))
-        nc.scalar.copy(out=bias_rows[:], in_=bias_ps[:])
-        regroup_k(0, 1)
-        regroup_k(1, 0)
-        regroup_k(1, 1)
+        nc.scalar.copy(out=bias_v_rows[:], in_=bias_ps[:, 0:PACK, :])
+        regroup_v(nc.scalar.copy, 1)
+        nc.scalar.copy(out=bias_q_rows[:], in_=bias_ps[:, PACK : 2 * PACK, :])
+        regroup_k(nc.scalar.copy, 0, 0)
+        regroup_k(nc.scalar.copy, 0, 1)
+        regroup_k(nc.scalar.copy, 1, 0)
 
-        regroup_v(nc.vector.tensor_copy, slice(0, HALF))
-        quantise(v_codes[:], v_scales[:], grouped_v[:].rearrange("p w t -> p (w t)"))
-        quantise(x_codes[:], x_scales[:], x_grouped[:].rearrange("p r t -> p (r t)"))
-        regroup_q(0)
-        regroup_q(1)
+        acc = {}
 
-        def project(name, h, codes, scales, bias, out_dram):
-            acc = psum.tile([P, HALF], F32, name="acc_%s%d" % (name, h))
-            multiply(acc[:], x_codes[:], x_scales[:], codes, scales)
+        def product(name, h):
+            acc[name, h] = psum.tile([P, HALF], F32, name="acc_%s%d" % (name, h))
+            multiply(acc[name, h][:], x_codes[:], x_scales[:], codes[name, h][:], scales[name, h][:])
+
+        def finish(name, h, bias, out_dram):
             width = bias.shape[2]
             result = keep.tile([P, HALF], F32, name="%s_sb%d" % (name, h))
             nc.vector.tensor_tensor(
                 out=result[:].rearrange("r (m c) -> r m c", c=width),
-                in0=acc[:].rearrange("r (m c) -> r m c", c=width),
+                in0=acc[name, h][:].rearrange("r (m c) -> r m c", c=width),
                 in1=bias,
                 op=ALU.add,
             )
@@ -198,35 +199,70 @@ def tile_relational_s_kernel(tc, inp, gamma, beta, W_qk, b_qk, W_v, b_v, out_0, 
                     in_=result[b * NE : (b + 1) * NE, :].rearrange("n (h j) -> n h j", j=HD),
                 )
 
-        def bias_of_v(h):
-            return bias_rows[:, 0:PACK, h * NE : (h + 1) * NE].rearrange("r t p -> r p t")
+        def finish_v(h):
+            finish("v", h, bias_v_rows[:, :, h * NE : (h + 1) * NE].rearrange("r t p -> r p t"), out_2)
 
-        def bias_of_q(h):
-            return bias_rows[:, PACK + 2 * h : PACK + 2 * h + 2, :].rearrange("r c m -> r m c")
+        def finish_q(h):
+            finish("q", h, bias_q_rows[:, 2 * h : 2 * h + 2, :].rearrange("r c m -> r m c"), out_0)
 
-        for h in range(2):
-            cols = slice(h * HALF, (h + 1) * HALF)
-            project("v", h, v_codes[:, cols], v_scales[:, cols], bias_of_v(h), out_2)
-            quantise(q_codes[h][:], q_scales[h][:], grouped_q[h][:].rearrange("p f t -> p (f t)"))
-        for h in range(2):
-            project("q", h, q_codes[h][:], q_scales[h][:], bias_of_q(h), out_0)
-            quantise(k_codes[h][:], k_scales[h][:], grouped_k[h][:].rearrange("p c m t -> p (c m t)"))
+        regroup_q(nc.vector.tensor_copy, 0)
+        quantise_w("v", 0)
+        quantise(x_codes[:], x_scales[:], x_grouped[:].rearrange("p r t -> p (r t)"))
+        product("v", 0)
+        quantise_w("q", 0)
+        product("q", 0)
+        finish_v(0)
+        regroup_q(nc.vector.tensor_copy, 1)
+        quantise_w("v", 1)
+        product("v", 1)
+        finish_q(0)
+        quantise_w("q", 1)
+        product("q", 1)
+        finish_v(1)
+        regroup_k(nc.vector.tensor_copy, 1, 1)
+        quantise_w("k", 0)
 
         k_dram = out_1.rearrange("b h j n -> b (h j) n")
+        k_sb = []
         for h in range(2):
-            k_sb = keep.tile([P, BATCH, 2, NE], F32, name="k_sb%d" % h)
-            for c in range(2):
-                acc_k = psum.tile([P, P], F32, name="acc_k%d%d" % (h, c), tag="bank%d" % (2 * h + c))
-                m_cols = slice(c * P, (c + 1) * P)
-                multiply(acc_k[:], k_codes[h][:, m_cols], k_scales[h][:, m_cols], x_codes[:], x_scales[:])
-                nc.scalar.activation(
-                    out=k_sb[:, :, c, :],
-                    in_=acc_k[:].rearrange("m (b n) -> m b n", b=BATCH),
-                    func=ACT.Identity,
-                    bias=bias_k[:, h, c : c + 1],
-                    scale=1.0,
-                )
+            k_sb.append(keep.tile([P, BATCH, 2, NE], F32, name="k_sb%d" % h))
+
+        def product_k(h, c):
+            acc["k", h, c] = psum.tile([P, P], F32, name="acc_k%d%d" % (h, c), tag="bank%d" % (2 * h + c))
+            m_cols = slice(c * P, (c + 1) * P)
+            multiply(acc["k", h, c][:], codes["k", h][:, m_cols], scales["k", h][:, m_cols], x_codes[:], x_scales[:])
+
+        def finish_k_scalar(h, c):
+            nc.scalar.activation(
+                out=k_sb[h][:, :, c, :],
+                in_=acc["k", h, c][:].rearrange("m (b n) -> m b n", b=BATCH),
+                func=ACT.Identity,
+                bias=bias_k[:, h, c : c + 1],
+                scale=1.0,
+            )
+
+        def finish_k_vector(h, c):
+            nc.vector.tensor_scalar_add(
+                out=k_sb[h][:, :, c, :],
+                in0=acc["k", h, c][:].rearrange("m (b n) -> m b n", b=BATCH),
+                scalar1=bias_k[:, h, c : c + 1],
+            )
+
+        def store_k(h):
             nc.sync.dma_start(
                 out=k_dram[:, h * HALF : (h + 1) * HALF, :].rearrange("b (m c) n -> m b (c n)", c=2),
-                in_=k_sb[:].rearrange("m b c n -> m b (c n)"),
+                in_=k_sb[h][:].rearrange("m b c n -> m b (c n)"),
             )
+
+        product_k(0, 0)
+        product_k(0, 1)
+        finish_q(1)
+        quantise_w("k", 1)
+        product_k(1, 0)
+        product_k(1, 1)
+        finish_k_scalar(0, 0)
+        finish_k_scalar(0, 1)
+        store_k(0)
+        finish_k_scalar(1, 0)
+        finish_k_vector(1, 1)
+        store_k(1)

@@ -35,6 +35,14 @@ def tile_relational_s_kernel(tc, inp, gamma, beta, W_qk, b_qk, W_v, b_v, out_0, 
         def row_on_all_partitions(out, column):
             nc.tensor.transpose(out, column.to_broadcast([P, P]), ident[:])
 
+        def words_on_all_partitions(out, vector_cols):
+            words = vector_cols.bitcast(F32)
+            for u in range(2):
+                nc.tensor.transpose(out[:, u, :], words[:, u : u + 1].to_broadcast([P, P]), ident_words[:])
+
+        def as_values(words):
+            return words.rearrange("r s p -> r (s p)").bitcast(BF16).rearrange("r (s p e) -> r s p e", p=P, e=2)
+
         def quantise(codes, scales, grouped):
             nc.vector.quantize_mx(out=codes.bitcast(FP8X4), scales=scales, in_=grouped)
 
@@ -76,6 +84,8 @@ def tile_relational_s_kernel(tc, inp, gamma, beta, W_qk, b_qk, W_v, b_v, out_0, 
 
         ident = keep.tile([P, P], BF16)
         make_identity(nc, ident[:])
+        ident_words = keep.tile([P, P], F32)
+        make_identity(nc, ident_words[:])
         zero = keep.tile([P, 1], F32)
         nc.gpsimd.memset(zero[:], 0.0)
         eps = keep.tile([P, 1], F32)
@@ -87,12 +97,17 @@ def tile_relational_s_kernel(tc, inp, gamma, beta, W_qk, b_qk, W_v, b_v, out_0, 
             out=bias_k[:], in_=b_qk_cols[:].rearrange("m h (c e) -> m e h c", e=2)[:, 1]
         )
 
-        gamma_rows = psum.tile([P, PACK, P], BF16, tag="bank0")
-        for t in range(PACK):
-            row_on_all_partitions(gamma_rows[:, t, :], gamma_cols[:, t : t + 1])
-        beta_rows = psum.tile([P, PACK, P], BF16, tag="bank1")
-        for t in range(PACK):
-            row_on_all_partitions(beta_rows[:, t, :], beta_cols[:, t : t + 1])
+        scale_shift = psum.tile([P, 4, P], F32, tag="bank0")
+        words_on_all_partitions(scale_shift[:, 0:2, :], gamma_cols[:])
+        words_on_all_partitions(scale_shift[:, 2:4, :], beta_cols[:])
+        gamma_rows = as_values(scale_shift[:])[:, 0:2]
+        beta_rows = as_values(scale_shift[:])[:, 2:4]
+        bias_v_ps = psum.tile([P, 2, P], F32, tag="bank1")
+        words_on_all_partitions(bias_v_ps[:], b_v_cols[:])
+        bias_q_ps = psum.tile([P, PACK, P], BF16, tag="bank2")
+        for h in range(2):
+            for c in range(2):
+                row_on_all_partitions(bias_q_ps[:, 2 * h + c, :], b_qk_cols[:, h, 2 * c : 2 * c + 1])
 
         stats = keep.tile([P, 6], F32)
         nc.vector.bn_stats(out=stats[:], in_=x_in[:])
@@ -100,37 +115,30 @@ def tile_relational_s_kernel(tc, inp, gamma, beta, W_qk, b_qk, W_v, b_v, out_0, 
         nc.vector.bn_aggr(out=mean_var[:], in_=stats[:])
         std = keep.tile([P, 1], F32)
         nc.scalar.activation(out=std[:], in_=mean_var[:, 1:2], func=ACT.Sqrt, bias=eps[:], scale=1.0)
-        centred = keep.tile([P, PACK, P], F32)
-        nc.vector.scalar_tensor_tensor(
-            out=centred[:],
-            in0=x_in[:].rearrange("r (p t) -> r t p", t=PACK),
-            scalar=mean_var[:, 0:1],
-            in1=gamma_rows[:],
-            op0=ALU.subtract,
-            op1=ALU.mult,
-        )
+        centred = keep.tile([P, 2, P, 2], F32)
+        for u in range(2):
+            nc.vector.scalar_tensor_tensor(
+                out=centred[:, u],
+                in0=x_in[:].rearrange("r (p u e) -> r u p e", u=2, e=2)[:, u],
+                scalar=mean_var[:, 0:1],
+                in1=gamma_rows[:, u],
+                op0=ALU.subtract,
+                op1=ALU.mult,
+            )
         rstd = keep.tile([P, 1], F32)
         nc.vector.reciprocal(out=rstd[:], in_=std[:])
-        x_bf = keep.tile([P, PACK, P], BF16)
-        x_t = psum.tile([P, PACK, P], BF16, tag="bank3")
-        for first in range(0, PACK, 2):
-            pair = slice(first, first + 2)
+        x_bf = keep.tile([P, 2, P, 2], BF16)
+        x_t = psum.tile([P, 2, P], F32, tag="bank3")
+        for u in range(2):
             nc.vector.scalar_tensor_tensor(
-                out=x_bf[:, pair, :],
-                in0=centred[:, pair, :],
+                out=x_bf[:, u],
+                in0=centred[:, u],
                 scalar=rstd[:],
-                in1=beta_rows[:, pair, :],
+                in1=beta_rows[:, u],
                 op0=ALU.mult,
                 op1=ALU.add,
             )
-            for t in range(first, first + 2):
-                nc.tensor.transpose(x_t[:, t, :], x_bf[:, t, :], ident[:])
-        bias_ps = psum.tile([P, 2 * PACK, P], BF16, tag="bank2")
-        for t in range(PACK):
-            row_on_all_partitions(bias_ps[:, t, :], b_v_cols[:, t : t + 1])
-        for h in range(2):
-            for c in range(2):
-                row_on_all_partitions(bias_ps[:, PACK + 2 * h + c, :], b_qk_cols[:, h, 2 * c : 2 * c + 1])
+            nc.tensor.transpose(x_t[:, u, :], x_bf[:, u].rearrange("r p e -> r (p e)").bitcast(F32), ident_words[:])
 
         x_grouped = keep.tile([P, P, PACK], BF16, align_bytes=64)
         x_codes = keep.tile([P, P], U32, align_bytes=64)
@@ -166,14 +174,17 @@ def tile_relational_s_kernel(tc, inp, gamma, beta, W_qk, b_qk, W_v, b_v, out_0, 
         def quantise_w(name, h):
             quantise(codes[name, h][:], scales[name, h][:], grouped[name, h][:].rearrange("p f t -> p (f t)"))
 
-        bias_v_rows = keep.tile([P, PACK, P], BF16)
+        bias_v_rows = keep.tile([P, P, 2], F32)
         bias_q_rows = keep.tile([P, PACK, P], BF16)
 
         regroup_v(nc.scalar.copy, 0)
-        nc.scalar.copy(out=x_grouped[:], in_=x_t[:].rearrange("p t r -> p r t"))
-        nc.scalar.copy(out=bias_v_rows[:], in_=bias_ps[:, 0:PACK, :])
+        nc.scalar.copy(out=bias_v_rows[:], in_=bias_v_ps[:].rearrange("r u p -> r p u"))
+        nc.scalar.copy(
+            out=x_grouped[:].rearrange("p r t -> p (r t)").bitcast(F32).rearrange("p (r u) -> p r u", u=2),
+            in_=x_t[:].rearrange("p u r -> p r u"),
+        )
         regroup_v(nc.scalar.copy, 1)
-        nc.scalar.copy(out=bias_q_rows[:], in_=bias_ps[:, PACK : 2 * PACK, :])
+        nc.scalar.copy(out=bias_q_rows[:], in_=bias_q_ps[:])
         regroup_k(nc.scalar.copy, 0, 0)
         regroup_k(nc.scalar.copy, 0, 1)
         regroup_k(nc.scalar.copy, 1, 0)
@@ -184,14 +195,10 @@ def tile_relational_s_kernel(tc, inp, gamma, beta, W_qk, b_qk, W_v, b_v, out_0, 
             acc[name, h] = psum.tile([P, HALF], F32, name="acc_%s%d" % (name, h))
             multiply(acc[name, h][:], x_codes[:], x_scales[:], codes[name, h][:], scales[name, h][:])
 
-        def finish(name, h, bias, out_dram):
-            width = bias.shape[2]
+        def finish(name, h, in_bias_order, bias, out_dram):
             result = keep.tile([P, HALF], F32, name="%s_sb%d" % (name, h))
             nc.vector.tensor_tensor(
-                out=result[:].rearrange("r (m c) -> r m c", c=width),
-                in0=acc[name, h][:].rearrange("r (m c) -> r m c", c=width),
-                in1=bias,
-                op=ALU.add,
+                out=in_bias_order(result[:]), in0=in_bias_order(acc[name, h][:]), in1=bias, op=ALU.add
             )
             for b in range(BATCH):
                 nc.sync.dma_start(
@@ -200,10 +207,22 @@ def tile_relational_s_kernel(tc, inp, gamma, beta, W_qk, b_qk, W_v, b_v, out_0, 
                 )
 
         def finish_v(h):
-            finish("v", h, bias_v_rows[:, :, h * NE : (h + 1) * NE].rearrange("r t p -> r p t"), out_2)
+            finish(
+                "v",
+                h,
+                lambda piece: piece,
+                bias_v_rows[:].rearrange("r p u -> r (p u)").bitcast(BF16)[:, h * HALF : (h + 1) * HALF],
+                out_2,
+            )
 
         def finish_q(h):
-            finish("q", h, bias_q_rows[:, 2 * h : 2 * h + 2, :].rearrange("r c m -> r m c"), out_0)
+            finish(
+                "q",
+                h,
+                lambda piece: piece.rearrange("r (m c) -> r m c", c=2),
+                bias_q_rows[:, 2 * h : 2 * h + 2, :].rearrange("r c m -> r m c"),
+                out_0,
+            )
 
         regroup_q(nc.vector.tensor_copy, 0)
         quantise_w("v", 0)

@@ -32,9 +32,6 @@ def tile_relational_s_kernel(tc, inp, gamma, beta, W_qk, b_qk, W_v, b_v, out_0, 
         psum = ctx.enter_context(tc.psum_pool(name="psum", bufs=1))
         ctx.enter_context(tc.manual_schedule())
 
-        def row_on_all_partitions(out, column):
-            nc.tensor.transpose(out, column.to_broadcast([P, P]), ident[:])
-
         def words_on_all_partitions(out, vector_cols):
             words = vector_cols.bitcast(F32)
             for u in range(2):
@@ -82,8 +79,6 @@ def tile_relational_s_kernel(tc, inp, gamma, beta, W_qk, b_qk, W_v, b_v, out_0, 
             )
             raw_qk.append(raw_h)
 
-        ident = keep.tile([P, P], BF16)
-        make_identity(nc, ident[:])
         ident_words = keep.tile([P, P], F32)
         make_identity(nc, ident_words[:])
         zero = keep.tile([P, 1], F32)
@@ -92,6 +87,10 @@ def tile_relational_s_kernel(tc, inp, gamma, beta, W_qk, b_qk, W_v, b_v, out_0, 
         nc.vector.tensor_scalar_add(out=eps[:], in0=zero[:], scalar1=LN_EPS)
         warm = keep.tile([P, 1], F32)
         nc.scalar.activation(out=warm[:], in_=eps[:], func=ACT.Sqrt)
+        b_q_cols = keep.tile([P, 2, 2], BF16)
+        nc.gpsimd.tensor_copy(
+            out=b_q_cols[:], in_=b_qk_cols[:].rearrange("m h (c e) -> m e h c", e=2)[:, 0]
+        )
         bias_k = keep.tile([P, 2, 2], F32)
         nc.gpsimd.tensor_copy(
             out=bias_k[:], in_=b_qk_cols[:].rearrange("m h (c e) -> m e h c", e=2)[:, 1]
@@ -104,10 +103,6 @@ def tile_relational_s_kernel(tc, inp, gamma, beta, W_qk, b_qk, W_v, b_v, out_0, 
         beta_rows = as_values(scale_shift[:])[:, 2:4]
         bias_v_ps = psum.tile([P, 2, P], F32, tag="bank1")
         words_on_all_partitions(bias_v_ps[:], b_v_cols[:])
-        bias_q_ps = psum.tile([P, PACK, P], BF16, tag="bank2")
-        for h in range(2):
-            for c in range(2):
-                row_on_all_partitions(bias_q_ps[:, 2 * h + c, :], b_qk_cols[:, h, 2 * c : 2 * c + 1])
 
         stats = keep.tile([P, 6], F32)
         nc.vector.bn_stats(out=stats[:], in_=x_in[:])
@@ -139,6 +134,8 @@ def tile_relational_s_kernel(tc, inp, gamma, beta, W_qk, b_qk, W_v, b_v, out_0, 
                 op1=ALU.add,
             )
             nc.tensor.transpose(x_t[:, u, :], x_bf[:, u].rearrange("r p e -> r (p e)").bitcast(F32), ident_words[:])
+        bias_q_ps = psum.tile([P, 2, P], F32, tag="bank2")
+        words_on_all_partitions(bias_q_ps[:], b_q_cols[:].rearrange("m h c -> m (h c)"))
 
         x_grouped = keep.tile([P, P, PACK], BF16, align_bytes=64)
         x_codes = keep.tile([P, P], U32, align_bytes=64)
@@ -175,7 +172,16 @@ def tile_relational_s_kernel(tc, inp, gamma, beta, W_qk, b_qk, W_v, b_v, out_0, 
             quantise(codes[name, h][:], scales[name, h][:], grouped[name, h][:].rearrange("p f t -> p (f t)"))
 
         bias_v_rows = keep.tile([P, P, 2], F32)
-        bias_q_rows = keep.tile([P, PACK, P], BF16)
+        bias_q_rows = keep.tile([P, 2, P], F32)
+
+        nc.gpsimd.tensor_scalar(
+            out=grouped["v", 1][:],
+            in0=raw_v[1][:].rearrange("p t w -> p w t"),
+            scalar1=1.0,
+            scalar2=0.0,
+            op0=ALU.mult,
+            op1=ALU.add,
+        )
 
         regroup_v(nc.scalar.copy, 0)
         nc.scalar.copy(out=bias_v_rows[:], in_=bias_v_ps[:].rearrange("r u p -> r p u"))
@@ -183,11 +189,12 @@ def tile_relational_s_kernel(tc, inp, gamma, beta, W_qk, b_qk, W_v, b_v, out_0, 
             out=x_grouped[:].rearrange("p r t -> p (r t)").bitcast(F32).rearrange("p (r u) -> p r u", u=2),
             in_=x_t[:].rearrange("p u r -> p r u"),
         )
-        regroup_v(nc.scalar.copy, 1)
         nc.scalar.copy(out=bias_q_rows[:], in_=bias_q_ps[:])
+        regroup_q(nc.scalar.copy, 1)
         regroup_k(nc.scalar.copy, 0, 0)
         regroup_k(nc.scalar.copy, 0, 1)
         regroup_k(nc.scalar.copy, 1, 0)
+        regroup_k(nc.scalar.copy, 1, 1)
 
         acc = {}
 
@@ -219,8 +226,8 @@ def tile_relational_s_kernel(tc, inp, gamma, beta, W_qk, b_qk, W_v, b_v, out_0, 
             finish(
                 "q",
                 h,
-                lambda piece: piece.rearrange("r (m c) -> r m c", c=2),
-                bias_q_rows[:, 2 * h : 2 * h + 2, :].rearrange("r c m -> r m c"),
+                lambda piece: piece,
+                bias_q_rows[:].rearrange("r h m -> r (h m)").bitcast(BF16)[:, h * HALF : (h + 1) * HALF],
                 out_0,
             )
 
@@ -231,14 +238,12 @@ def tile_relational_s_kernel(tc, inp, gamma, beta, W_qk, b_qk, W_v, b_v, out_0, 
         quantise_w("q", 0)
         product("q", 0)
         finish_v(0)
-        regroup_q(nc.vector.tensor_copy, 1)
         quantise_w("v", 1)
         product("v", 1)
         finish_q(0)
         quantise_w("q", 1)
         product("q", 1)
         finish_v(1)
-        regroup_k(nc.vector.tensor_copy, 1, 1)
         quantise_w("k", 0)
 
         k_dram = out_1.rearrange("b h j n -> b (h j) n")

@@ -273,10 +273,11 @@ def tile_relational_s_kernel(tc, inp, gamma, beta, W_qk, b_qk, W_v, b_v, out_0, 
             )
 
         def store_k(h):
-            nc.sync.dma_start(
-                out=k_dram[:, h * HALF : (h + 1) * HALF, :].rearrange("b (m c) n -> m b (c n)", c=2),
-                in_=k_sb[h][:].rearrange("m b c n -> m b (c n)"),
-            )
+            for b in range(BATCH):
+                nc.sync.dma_start(
+                    out=k_dram[b, h * HALF : (h + 1) * HALF, :].rearrange("(m c) n -> m (c n)", c=2),
+                    in_=k_sb[h][:, b].rearrange("m c n -> m (c n)"),
+                )
 
         product_k(0, 0)
         product_k(0, 1)

@@ -111,7 +111,9 @@ def tile_relational_s_kernel(tc, inp, gamma, beta, W_qk, b_qk, W_v, b_v, out_0, 
         std = keep.tile([P, 1], F32)
         nc.scalar.activation(out=std[:], in_=mean_var[:, 1:2], func=ACT.Sqrt, bias=eps[:], scale=1.0)
         centred = keep.tile([P, 2, P, 2], F32)
-        for u in range(2):
+        rstd = keep.tile([P, 1], F32)
+
+        def centre(u):
             nc.vector.scalar_tensor_tensor(
                 out=centred[:, u],
                 in0=x_in[:].rearrange("r (p u e) -> r u p e", u=2, e=2)[:, u],
@@ -120,8 +122,10 @@ def tile_relational_s_kernel(tc, inp, gamma, beta, W_qk, b_qk, W_v, b_v, out_0, 
                 op0=ALU.subtract,
                 op1=ALU.mult,
             )
-        rstd = keep.tile([P, 1], F32)
+
+        centre(0)
         nc.vector.reciprocal(out=rstd[:], in_=std[:])
+        centre(1)
         x_bf = keep.tile([P, 2, P, 2], BF16)
         x_t = psum.tile([P, 2, P], F32, tag="bank3")
         for u in range(2):
@@ -175,26 +179,25 @@ def tile_relational_s_kernel(tc, inp, gamma, beta, W_qk, b_qk, W_v, b_v, out_0, 
         bias_q_rows = keep.tile([P, 2, P], F32)
 
         nc.gpsimd.tensor_scalar(
-            out=grouped["v", 1][:],
-            in0=raw_v[1][:].rearrange("p t w -> p w t"),
+            out=grouped["v", 0][:],
+            in0=raw_v[0][:].rearrange("p t w -> p w t"),
             scalar1=1.0,
             scalar2=0.0,
             op0=ALU.mult,
             op1=ALU.add,
         )
 
-        regroup_v(nc.scalar.copy, 0)
         nc.scalar.copy(out=bias_v_rows[:], in_=bias_v_ps[:].rearrange("r u p -> r p u"))
+        regroup_v(nc.scalar.copy, 1)
+        regroup_k(nc.scalar.copy, 0, 0)
         nc.scalar.copy(
             out=x_grouped[:].rearrange("p r t -> p (r t)").bitcast(F32).rearrange("p (r u) -> p r u", u=2),
             in_=x_t[:].rearrange("p u r -> p r u"),
         )
         nc.scalar.copy(out=bias_q_rows[:], in_=bias_q_ps[:])
         regroup_q(nc.scalar.copy, 1)
-        regroup_k(nc.scalar.copy, 0, 0)
         regroup_k(nc.scalar.copy, 0, 1)
         regroup_k(nc.scalar.copy, 1, 0)
-        regroup_k(nc.scalar.copy, 1, 1)
 
         acc = {}
 
@@ -231,21 +234,6 @@ def tile_relational_s_kernel(tc, inp, gamma, beta, W_qk, b_qk, W_v, b_v, out_0, 
                 out_0,
             )
 
-        regroup_q(nc.vector.tensor_copy, 0)
-        quantise_w("v", 0)
-        quantise(x_codes[:], x_scales[:], x_grouped[:].rearrange("p r t -> p (r t)"))
-        product("v", 0)
-        quantise_w("q", 0)
-        product("q", 0)
-        finish_v(0)
-        quantise_w("v", 1)
-        product("v", 1)
-        finish_q(0)
-        quantise_w("q", 1)
-        product("q", 1)
-        finish_v(1)
-        quantise_w("k", 0)
-
         k_dram = out_1.rearrange("b h j n -> b (h j) n")
         k_sb = []
         for h in range(2):
@@ -279,12 +267,27 @@ def tile_relational_s_kernel(tc, inp, gamma, beta, W_qk, b_qk, W_v, b_v, out_0, 
                     in_=k_sb[h][:, b].rearrange("m c n -> m (c n)"),
                 )
 
+        regroup_q(nc.vector.tensor_copy, 0)
+        quantise_w("v", 0)
+        quantise_w("v", 1)
+        quantise(x_codes[:], x_scales[:], x_grouped[:].rearrange("p r t -> p (r t)"))
+        product("v", 0)
+        product("v", 1)
+        quantise_w("q", 0)
+        product("q", 0)
+        regroup_k(nc.vector.tensor_copy, 1, 1)
+        finish_v(0)
+        finish_v(1)
+        quantise_w("q", 1)
+        product("q", 1)
+        finish_q(0)
+        quantise_w("k", 0)
         product_k(0, 0)
         product_k(0, 1)
-        finish_q(1)
         quantise_w("k", 1)
         product_k(1, 0)
         product_k(1, 1)
+        finish_q(1)
         finish_k_scalar(0, 0)
         finish_k_scalar(0, 1)
         store_k(0)

@@ -20,6 +20,9 @@ HD = 32
 HALF = 256
 HEADS = HALF // HD
 RUN = 4
+PARITIES = 2
+PAIRS = NE // PARITIES
+X_BLOCKS = 2 * PARITIES + 1
 LN_EPS = 1e-5
 
 FLOPS = 2 * P * D * (3 * D)
@@ -87,6 +90,15 @@ def tile_relational_s_kernel(tc, inp, gamma, beta, W_qk, b_qk, W_v, b_v, out_0, 
         nc.vector.tensor_scalar_add(out=eps[:], in0=zero[:], scalar1=LN_EPS)
         warm = keep.tile([P, 1], F32)
         nc.scalar.activation(out=warm[:], in_=eps[:], func=ACT.Sqrt)
+        x_grouped = keep.tile([P, PARITIES, NE, PACK], BF16, align_bytes=64)
+        x_codes = keep.tile([P, X_BLOCKS * NE], U32, align_bytes=64)
+        x_scales = keep.tile([P, X_BLOCKS * NE], U8, align_bytes=64)
+        nc.gpsimd.memset(x_codes[:].rearrange("p (s n) -> p s n", n=NE)[:, 0::2, :], 0)
+        nc.gpsimd.memset(x_scales[:].rearrange("p (s n) -> p s n", n=NE)[:, 0::2, :], 127)
+
+        def x_block(a):
+            return slice((2 * a + 1) * NE, (2 * a + 2) * NE)
+
         b_q_cols = keep.tile([P, 2, 2], BF16)
         nc.gpsimd.tensor_copy(
             out=b_q_cols[:], in_=b_qk_cols[:].rearrange("m h (c e) -> m e h c", e=2)[:, 0]
@@ -141,10 +153,6 @@ def tile_relational_s_kernel(tc, inp, gamma, beta, W_qk, b_qk, W_v, b_v, out_0, 
         bias_q_ps = psum.tile([P, 2, P], F32, tag="bank2")
         words_on_all_partitions(bias_q_ps[:], b_q_cols[:].rearrange("m h c -> m (h c)"))
 
-        x_grouped = keep.tile([P, P, PACK], BF16, align_bytes=64)
-        x_codes = keep.tile([P, P], U32, align_bytes=64)
-        x_scales = keep.tile([P, P], U8, align_bytes=64)
-
         grouped = {}
         codes = {}
         scales = {}
@@ -175,8 +183,8 @@ def tile_relational_s_kernel(tc, inp, gamma, beta, W_qk, b_qk, W_v, b_v, out_0, 
         def quantise_w(name, h):
             quantise(codes[name, h][:], scales[name, h][:], grouped[name, h][:].rearrange("p f t -> p (f t)"))
 
-        bias_v_rows = keep.tile([P, P, 2], F32)
-        bias_q_rows = keep.tile([P, 2, P], F32)
+        bias_v_rows = keep.tile([P, NE, 2], F32)
+        bias_q_rows = keep.tile([P, P], F32)
 
         nc.gpsimd.tensor_scalar(
             out=grouped["v", 0][:],
@@ -187,52 +195,58 @@ def tile_relational_s_kernel(tc, inp, gamma, beta, W_qk, b_qk, W_v, b_v, out_0, 
             op1=ALU.add,
         )
 
-        nc.scalar.copy(out=bias_v_rows[:], in_=bias_v_ps[:].rearrange("r u p -> r p u"))
+        for s in range(2):
+            half = slice(s * NE, (s + 1) * NE)
+            nc.scalar.copy(out=bias_v_rows[half, :, :], in_=bias_v_ps[half, :, half].rearrange("r u p -> r p u"))
         regroup_v(nc.scalar.copy, 1)
         regroup_k(nc.scalar.copy, 0, 0)
         nc.scalar.copy(
-            out=x_grouped[:].rearrange("p r t -> p (r t)").bitcast(F32).rearrange("p (r u) -> p r u", u=2),
-            in_=x_t[:].rearrange("p u r -> p r u"),
+            out=x_grouped[:]
+            .rearrange("p a m t -> p (a m t)")
+            .bitcast(F32)
+            .rearrange("p (a m u) -> p a m u", a=PARITIES, u=2),
+            in_=x_t[:].rearrange("p u (m a) -> p a m u", a=PARITIES),
         )
-        nc.scalar.copy(out=bias_q_rows[:], in_=bias_q_ps[:])
+        for s in range(2):
+            half = slice(s * NE, (s + 1) * NE)
+            nc.scalar.copy(out=bias_q_rows[half, :], in_=bias_q_ps[half, s, :])
         regroup_q(nc.scalar.copy, 1)
         regroup_k(nc.scalar.copy, 0, 1)
-        regroup_k(nc.scalar.copy, 1, 0)
 
         acc = {}
 
-        def product(name, h):
-            acc[name, h] = psum.tile([P, HALF], F32, name="acc_%s%d" % (name, h))
-            multiply(acc[name, h][:], x_codes[:], x_scales[:], codes[name, h][:], scales[name, h][:])
+        def product(name):
+            acc[name] = psum.tile([P, PARITIES, HALF], F32, name="acc_%s" % name)
+            for a in range(PARITIES):
+                for s in range(2):
+                    start_col = (2 * a + 1 - s) * NE
+                    window = slice(start_col, start_col + P)
+                    nc.tensor.matmul_mx(
+                        out=acc[name][:, a, :],
+                        lhsT=x_codes[:, window].bitcast(FP8X4),
+                        lhsT_scale=x_scales[:, window],
+                        rhs=codes[name, s][:].bitcast(FP8X4),
+                        rhs_scale=scales[name, s][:],
+                        start=(s == 0),
+                        stop=(s == 1),
+                    )
 
-        def finish(name, h, in_bias_order, bias, out_dram):
-            result = keep.tile([P, HALF], F32, name="%s_sb%d" % (name, h))
-            nc.vector.tensor_tensor(
-                out=in_bias_order(result[:]), in0=in_bias_order(acc[name, h][:]), in1=bias, op=ALU.add
-            )
-            for b in range(BATCH):
-                nc.sync.dma_start(
-                    out=out_dram[b, h * HEADS : (h + 1) * HEADS].rearrange("h n j -> n h j"),
-                    in_=result[b * NE : (b + 1) * NE, :].rearrange("n (h j) -> n h j", j=HD),
+        def finish(name, bias, out_dram):
+            result = keep.tile([P, HEADS, PARITIES, HD], F32, name="%s_sb" % name)
+            for a in range(PARITIES):
+                nc.vector.tensor_tensor(
+                    out=result[:, :, a, :],
+                    in0=acc[name][:, a, :].rearrange("r (h j) -> r h j", j=HD),
+                    in1=bias.rearrange("r (h j) -> r h j", j=HD),
+                    op=ALU.add,
                 )
-
-        def finish_v(h):
-            finish(
-                "v",
-                h,
-                lambda piece: piece,
-                bias_v_rows[:].rearrange("r p u -> r (p u)").bitcast(BF16)[:, h * HALF : (h + 1) * HALF],
-                out_2,
-            )
-
-        def finish_q(h):
-            finish(
-                "q",
-                h,
-                lambda piece: piece,
-                bias_q_rows[:].rearrange("r h m -> r (h m)").bitcast(BF16)[:, h * HALF : (h + 1) * HALF],
-                out_0,
-            )
+            for s in range(2):
+                for b in range(BATCH):
+                    rows = s * NE + b * PAIRS
+                    nc.sync.dma_start(
+                        out=out_dram[b, s * HEADS : (s + 1) * HEADS].rearrange("h (n a) j -> n h (a j)", a=PARITIES),
+                        in_=result[rows : rows + PAIRS, :, :, :].rearrange("n h a j -> n h (a j)"),
+                    )
 
         k_dram = out_1.rearrange("b h j n -> b (h j) n")
         k_sb = []
@@ -240,25 +254,30 @@ def tile_relational_s_kernel(tc, inp, gamma, beta, W_qk, b_qk, W_v, b_v, out_0, 
             k_sb.append(keep.tile([P, BATCH, 2, NE], F32, name="k_sb%d" % h))
 
         def product_k(h, c):
-            acc["k", h, c] = psum.tile([P, P], F32, name="acc_k%d%d" % (h, c), tag="bank%d" % (2 * h + c))
+            acc["k", h, c] = psum.tile([P, 2 * P], F32, name="acc_k%d%d" % (h, c), tag="bank%d" % (2 * h + c))
             m_cols = slice(c * P, (c + 1) * P)
-            multiply(acc["k", h, c][:], codes["k", h][:, m_cols], scales["k", h][:, m_cols], x_codes[:], x_scales[:])
+            x_cols = slice(NE, X_BLOCKS * NE)
+            multiply(
+                acc["k", h, c][:],
+                codes["k", h][:, m_cols],
+                scales["k", h][:, m_cols],
+                x_codes[:, x_cols],
+                x_scales[:, x_cols],
+            )
+
+        def k_in_order(h, c):
+            return acc["k", h, c][:].rearrange("m (a z b n) -> m z b n a", a=PARITIES, z=2, b=BATCH)[:, 0]
+
+        def k_place(h, c):
+            return k_sb[h][:, :, c, :].rearrange("m b (n a) -> m b n a", a=PARITIES)
 
         def finish_k_scalar(h, c):
             nc.scalar.activation(
-                out=k_sb[h][:, :, c, :],
-                in_=acc["k", h, c][:].rearrange("m (b n) -> m b n", b=BATCH),
-                func=ACT.Identity,
-                bias=bias_k[:, h, c : c + 1],
-                scale=1.0,
+                out=k_place(h, c), in_=k_in_order(h, c), func=ACT.Identity, bias=bias_k[:, h, c : c + 1], scale=1.0
             )
 
         def finish_k_vector(h, c):
-            nc.vector.tensor_scalar_add(
-                out=k_sb[h][:, :, c, :],
-                in0=acc["k", h, c][:].rearrange("m (b n) -> m b n", b=BATCH),
-                scalar1=bias_k[:, h, c : c + 1],
-            )
+            nc.vector.tensor_scalar_add(out=k_place(h, c), in0=k_in_order(h, c), scalar1=bias_k[:, h, c : c + 1])
 
         def store_k(h):
             for b in range(BATCH):
@@ -267,30 +286,28 @@ def tile_relational_s_kernel(tc, inp, gamma, beta, W_qk, b_qk, W_v, b_v, out_0, 
                     in_=k_sb[h][:, b].rearrange("m c n -> m (c n)"),
                 )
 
-        regroup_q(nc.vector.tensor_copy, 0)
         quantise_w("v", 0)
+        regroup_q(nc.vector.tensor_copy, 0)
         quantise_w("v", 1)
-        quantise(x_codes[:], x_scales[:], x_grouped[:].rearrange("p r t -> p (r t)"))
-        product("v", 0)
-        product("v", 1)
         quantise_w("q", 0)
-        product("q", 0)
+        for a in range(PARITIES):
+            quantise(x_codes[:, x_block(a)], x_scales[:, x_block(a)], x_grouped[:, a, :, :].rearrange("p m t -> p (m t)"))
+        product("v")
+        regroup_k(nc.vector.tensor_copy, 1, 0)
         regroup_k(nc.vector.tensor_copy, 1, 1)
-        finish_v(0)
-        finish_v(1)
-        quantise_w("q", 1)
-        product("q", 1)
-        finish_q(0)
-        quantise_w("k", 0)
-        product_k(0, 0)
-        product_k(0, 1)
         quantise_w("k", 1)
         product_k(1, 0)
         product_k(1, 1)
-        finish_q(1)
-        finish_k_scalar(0, 0)
-        finish_k_scalar(0, 1)
-        store_k(0)
+        finish("v", bias_v_rows[:].rearrange("r p u -> r (p u)").bitcast(BF16), out_2)
+        quantise_w("q", 1)
+        product("q")
         finish_k_scalar(1, 0)
-        finish_k_vector(1, 1)
+        finish_k_scalar(1, 1)
         store_k(1)
+        quantise_w("k", 0)
+        product_k(0, 0)
+        product_k(0, 1)
+        finish("q", bias_q_rows[:].bitcast(BF16), out_0)
+        finish_k_scalar(0, 0)
+        finish_k_vector(0, 1)
+        store_k(0)

@@ -195,11 +195,10 @@ def tile_relational_s_kernel(tc, inp, gamma, beta, W_qk, b_qk, W_v, b_v, out_0, 
             op1=ALU.add,
         )
 
+        regroup_v(nc.scalar.copy, 1)
         for s in range(2):
             half = slice(s * NE, (s + 1) * NE)
             nc.scalar.copy(out=bias_v_rows[half, :, :], in_=bias_v_ps[half, :, half].rearrange("r u p -> r p u"))
-        regroup_v(nc.scalar.copy, 1)
-        regroup_k(nc.scalar.copy, 0, 0)
         nc.scalar.copy(
             out=x_grouped[:]
             .rearrange("p a m t -> p (a m t)")
@@ -207,22 +206,23 @@ def tile_relational_s_kernel(tc, inp, gamma, beta, W_qk, b_qk, W_v, b_v, out_0, 
             .rearrange("p (a m u) -> p a m u", a=PARITIES, u=2),
             in_=x_t[:].rearrange("p u (m a) -> p a m u", a=PARITIES),
         )
+        regroup_q(nc.scalar.copy, 1)
         for s in range(2):
             half = slice(s * NE, (s + 1) * NE)
             nc.scalar.copy(out=bias_q_rows[half, :], in_=bias_q_ps[half, s, :])
-        regroup_q(nc.scalar.copy, 1)
+        regroup_k(nc.scalar.copy, 0, 0)
         regroup_k(nc.scalar.copy, 0, 1)
 
         acc = {}
 
         def product(name):
-            acc[name] = psum.tile([P, PARITIES, HALF], F32, name="acc_%s" % name)
             for a in range(PARITIES):
+                acc[name, a] = psum.tile([P, HALF], F32, name="acc_%s%d" % (name, a))
                 for s in range(2):
                     start_col = (2 * a + 1 - s) * NE
                     window = slice(start_col, start_col + P)
                     nc.tensor.matmul_mx(
-                        out=acc[name][:, a, :],
+                        out=acc[name, a][:],
                         lhsT=x_codes[:, window].bitcast(FP8X4),
                         lhsT_scale=x_scales[:, window],
                         rhs=codes[name, s][:].bitcast(FP8X4),
@@ -231,21 +231,29 @@ def tile_relational_s_kernel(tc, inp, gamma, beta, W_qk, b_qk, W_v, b_v, out_0, 
                         stop=(s == 1),
                     )
 
-        def finish(name, bias, out_dram):
-            result = keep.tile([P, HEADS, PARITIES, HD], F32, name="%s_sb" % name)
-            for a in range(PARITIES):
-                nc.vector.tensor_tensor(
-                    out=result[:, :, a, :],
-                    in0=acc[name][:, a, :].rearrange("r (h j) -> r h j", j=HD),
-                    in1=bias.rearrange("r (h j) -> r h j", j=HD),
-                    op=ALU.add,
-                )
-            for s in range(2):
-                for b in range(BATCH):
+        result = {}
+        for name in ("v", "q"):
+            result[name] = keep.tile([P, HEADS, PARITIES, HD], F32, name="%s_sb" % name)
+        bias_rows = {
+            "v": bias_v_rows[:].rearrange("r p u -> r (p u)").bitcast(BF16),
+            "q": bias_q_rows[:].bitcast(BF16),
+        }
+
+        def add_bias(name, a):
+            nc.vector.tensor_tensor(
+                out=result[name][:, :, a, :],
+                in0=acc[name, a][:].rearrange("r (h j) -> r h j", j=HD),
+                in1=bias_rows[name].rearrange("r (h j) -> r h j", j=HD),
+                op=ALU.add,
+            )
+
+        def store(name, out_dram):
+            for b in range(BATCH):
+                for s in range(2):
                     rows = s * NE + b * PAIRS
                     nc.sync.dma_start(
                         out=out_dram[b, s * HEADS : (s + 1) * HEADS].rearrange("h (n a) j -> n h (a j)", a=PARITIES),
-                        in_=result[rows : rows + PAIRS, :, :, :].rearrange("n h a j -> n h (a j)"),
+                        in_=result[name][rows : rows + PAIRS, :, :, :].rearrange("n h a j -> n h (a j)"),
                     )
 
         k_dram = out_1.rearrange("b h j n -> b (h j) n")
@@ -280,34 +288,37 @@ def tile_relational_s_kernel(tc, inp, gamma, beta, W_qk, b_qk, W_v, b_v, out_0, 
             nc.vector.tensor_scalar_add(out=k_place(h, c), in0=k_in_order(h, c), scalar1=bias_k[:, h, c : c + 1])
 
         def store_k(h):
-            for b in range(BATCH):
-                nc.sync.dma_start(
-                    out=k_dram[b, h * HALF : (h + 1) * HALF, :].rearrange("(m c) n -> m (c n)", c=2),
-                    in_=k_sb[h][:, b].rearrange("m c n -> m (c n)"),
-                )
+            nc.sync.dma_start(
+                out=k_dram[:, h * HALF : (h + 1) * HALF, :].rearrange("b (m c) n -> m b (c n)", c=2),
+                in_=k_sb[h][:].rearrange("m b c n -> m b (c n)"),
+            )
 
         quantise_w("v", 0)
         regroup_q(nc.vector.tensor_copy, 0)
         quantise_w("v", 1)
-        quantise_w("q", 0)
         for a in range(PARITIES):
             quantise(x_codes[:, x_block(a)], x_scales[:, x_block(a)], x_grouped[:, a, :, :].rearrange("p m t -> p (m t)"))
         product("v")
+        quantise_w("q", 0)
         regroup_k(nc.vector.tensor_copy, 1, 0)
         regroup_k(nc.vector.tensor_copy, 1, 1)
+        add_bias("v", 0)
+        quantise_w("q", 1)
+        product("q")
+        add_bias("v", 1)
+        store("v", out_2)
         quantise_w("k", 1)
         product_k(1, 0)
         product_k(1, 1)
-        finish("v", bias_v_rows[:].rearrange("r p u -> r (p u)").bitcast(BF16), out_2)
-        quantise_w("q", 1)
-        product("q")
-        finish_k_scalar(1, 0)
-        finish_k_scalar(1, 1)
-        store_k(1)
+        add_bias("q", 0)
+        add_bias("q", 1)
+        store("q", out_0)
         quantise_w("k", 0)
         product_k(0, 0)
         product_k(0, 1)
-        finish("q", bias_q_rows[:].bitcast(BF16), out_0)
+        finish_k_scalar(1, 0)
+        finish_k_scalar(1, 1)
+        store_k(1)
         finish_k_scalar(0, 0)
         finish_k_vector(0, 1)
         store_k(0)

@@ -174,10 +174,10 @@ def tile_relational_s_kernel(tc, inp, gamma, beta, W_qk, b_qk, W_v, b_v, out_0, 
                 in_=raw_qk[h][:].rearrange("p t (a i e) -> p e a t i", i=RUN, e=2)[:, 0],
             )
 
-        def regroup_k(copy, h, c):
+        def regroup_k(copy, h, m_cols):
             copy(
-                out=as_runs(grouped["k", h][:, c * P : (c + 1) * P, :]),
-                in_=raw_qk[h][:].rearrange("p t (a i c e) -> p c e a t i", i=RUN, c=2, e=2)[:, c, 1],
+                out=grouped["k", h][:].rearrange("p (c m) t -> p m t c", c=2)[:, m_cols],
+                in_=raw_qk[h][:].rearrange("p t (m c e) -> p e m t c", c=2, e=2)[:, 1, m_cols],
             )
 
         def quantise_w(name, h):
@@ -210,8 +210,7 @@ def tile_relational_s_kernel(tc, inp, gamma, beta, W_qk, b_qk, W_v, b_v, out_0, 
         for s in range(2):
             half = slice(s * NE, (s + 1) * NE)
             nc.scalar.copy(out=bias_q_rows[half, :], in_=bias_q_ps[half, s, :])
-        regroup_k(nc.scalar.copy, 0, 0)
-        regroup_k(nc.scalar.copy, 0, 1)
+        regroup_k(nc.scalar.copy, 0, slice(0, P))
 
         acc = {}
 
@@ -300,8 +299,7 @@ def tile_relational_s_kernel(tc, inp, gamma, beta, W_qk, b_qk, W_v, b_v, out_0, 
             quantise(x_codes[:, x_block(a)], x_scales[:, x_block(a)], x_grouped[:, a, :, :].rearrange("p m t -> p (m t)"))
         product("v")
         quantise_w("q", 0)
-        regroup_k(nc.vector.tensor_copy, 1, 0)
-        regroup_k(nc.vector.tensor_copy, 1, 1)
+        regroup_k(nc.vector.tensor_copy, 1, slice(0, P))
         add_bias("v", 0)
         quantise_w("q", 1)
         product("q")

from contextlib import ExitStack

import concourse.mybir as mybir
from concourse.masks import make_identity

BF16 = mybir.dt.bfloat16
F32 = mybir.dt.float32
U32 = mybir.dt.uint32
U8 = mybir.dt.uint8
FP8X4 = mybir.dt.float8_e4m3fn_x4
ALU = mybir.AluOpType
ACT = mybir.ActivationFunctionType

P = 128
PACK = 4
D = P * PACK
BATCH = 2
NE = 64
HD = 32
HALF = 256
HEADS = HALF // HD
RUN = 4
PARITIES = 2
PAIRS = NE // PARITIES
X_BLOCKS = 2 * PARITIES + 1
LN_EPS = 1e-5

FLOPS = 2 * P * D * (3 * D)


def tile_relational_s_kernel(tc, inp, gamma, beta, W_qk, b_qk, W_v, b_v, out_0, out_1, out_2):
    nc = tc.nc
    with ExitStack() as ctx:
        keep = ctx.enter_context(tc.tile_pool(name="keep", bufs=1))
        psum = ctx.enter_context(tc.psum_pool(name="psum", bufs=1))
        ctx.enter_context(tc.manual_schedule())

        def words_on_all_partitions(out, vector_cols):
            words = vector_cols.bitcast(F32)
            for u in range(2):
                nc.tensor.transpose(out[:, u, :], words[:, u : u + 1].to_broadcast([P, P]), ident_words[:])

        def as_values(words):
            return words.rearrange("r s p -> r (s p)").bitcast(BF16).rearrange("r (s p e) -> r s p e", p=P, e=2)

        def quantise(codes, scales, grouped):
            nc.vector.quantize_mx(out=codes.bitcast(FP8X4), scales=scales, in_=grouped)

        def multiply(out, lhsT, lhsT_scale, rhs, rhs_scale):
            nc.tensor.matmul_mx(
                out=out,
                lhsT=lhsT.bitcast(FP8X4),
                lhsT_scale=lhsT_scale,
                rhs=rhs.bitcast(FP8X4),
                rhs_scale=rhs_scale,
                start=True,
                stop=True,
            )

        x_in = keep.tile([P, D], BF16)
        nc.sync.dma_start(out=x_in[:], in_=inp.flatten_outer_dims())
        gamma_cols = keep.tile([P, PACK], BF16)
        nc.scalar.dma_start(out=gamma_cols[:], in_=gamma.rearrange("(p t) -> p t", t=PACK))
        beta_cols = keep.tile([P, PACK], BF16)
        nc.scalar.dma_start(out=beta_cols[:], in_=beta.rearrange("(p t) -> p t", t=PACK))
        b_v_cols = keep.tile([P, PACK], BF16)
        nc.sync.dma_start(out=b_v_cols[:], in_=b_v.rearrange("(p t) -> p t", t=PACK))
        b_qk_cols = keep.tile([P, 2, 4], BF16)
        nc.sync.dma_start(out=b_qk_cols[:], in_=b_qk.rearrange("(h m r) -> m h r", h=2, r=4))
        raw_v = []
        for h in range(2):
            raw_h = keep.tile([P, PACK, HALF], BF16, name="raw_v%d" % h)
            nc.sync.dma_start(
                out=raw_h[:], in_=W_v[:, h * HALF : (h + 1) * HALF].rearrange("(p t) w -> p t w", t=PACK)
            )
            raw_v.append(raw_h)
        raw_qk = []
        for h in range(2):
            raw_h = keep.tile([P, PACK, D], BF16, name="raw_qk%d" % h)
            nc.sync.dma_start(
                out=raw_h[:], in_=W_qk[:, h * D : (h + 1) * D].rearrange("(p t) w -> p t w", t=PACK)
            )
            raw_qk.append(raw_h)

        ident_words = keep.tile([P, P], F32)
        make_identity(nc, ident_words[:])
        zero = keep.tile([P, 1], F32)
        nc.gpsimd.memset(zero[:], 0.0)
        eps = keep.tile([P, 1], F32)
        nc.vector.tensor_scalar_add(out=eps[:], in0=zero[:], scalar1=LN_EPS)
        warm = keep.tile([P, 1], F32)
        nc.scalar.activation(out=warm[:], in_=eps[:], func=ACT.Sqrt)
        x_grouped = keep.tile([P, PARITIES, NE, PACK], BF16, align_bytes=64)
        x_codes = keep.tile([P, X_BLOCKS * NE], U32, align_bytes=64)
        x_scales = keep.tile([P, X_BLOCKS * NE], U8, align_bytes=64)
        nc.gpsimd.memset(x_codes[:].rearrange("p (s n) -> p s n", n=NE)[:, 0::2, :], 0)
        nc.gpsimd.memset(x_scales[:].rearrange("p (s n) -> p s n", n=NE)[:, 0::2, :], 127)

        def x_block(a):
            return slice((2 * a + 1) * NE, (2 * a + 2) * NE)

        b_q_cols = keep.tile([P, 2, 2], BF16)
        nc.gpsimd.tensor_copy(
            out=b_q_cols[:], in_=b_qk_cols[:].rearrange("m h (c e) -> m e h c", e=2)[:, 0]
        )
        bias_k = keep.tile([P, 2, 2], F32)
        nc.gpsimd.tensor_copy(
            out=bias_k[:], in_=b_qk_cols[:].rearrange("m h (c e) -> m e h c", e=2)[:, 1]
        )

        scale_shift = psum.tile([P, 4, P], F32, tag="bank0")
        words_on_all_partitions(scale_shift[:, 0:2, :], gamma_cols[:])
        words_on_all_partitions(scale_shift[:, 2:4, :], beta_cols[:])
        gamma_rows = as_values(scale_shift[:])[:, 0:2]
        beta_rows = as_values(scale_shift[:])[:, 2:4]
        bias_v_ps = psum.tile([P, 2, P], F32, tag="bank1")
        words_on_all_partitions(bias_v_ps[:], b_v_cols[:])

        stats = keep.tile([P, 6], F32)
        nc.vector.bn_stats(out=stats[:], in_=x_in[:])
        mean_var = keep.tile([P, 2], F32)
        nc.vector.bn_aggr(out=mean_var[:], in_=stats[:])
        std = keep.tile([P, 1], F32)
        nc.scalar.activation(out=std[:], in_=mean_var[:, 1:2], func=ACT.Sqrt, bias=eps[:], scale=1.0)
        centred = keep.tile([P, 2, P, 2], F32)
        rstd = keep.tile([P, 1], F32)

        def centre(u):
            nc.vector.scalar_tensor_tensor(
                out=centred[:, u],
                in0=x_in[:].rearrange("r (p u e) -> r u p e", u=2, e=2)[:, u],
                scalar=mean_var[:, 0:1],
                in1=gamma_rows[:, u],
                op0=ALU.subtract,
                op1=ALU.mult,
            )

        centre(0)
        nc.vector.reciprocal(out=rstd[:], in_=std[:])
        centre(1)
        x_bf = keep.tile([P, 2, P, 2], BF16)
        x_t = psum.tile([P, 2, P], F32, tag="bank3")
        for u in range(2):
            nc.vector.scalar_tensor_tensor(
                out=x_bf[:, u],
                in0=centred[:, u],
                scalar=rstd[:],
                in1=beta_rows[:, u],
                op0=ALU.mult,
                op1=ALU.add,
            )
            nc.tensor.transpose(x_t[:, u, :], x_bf[:, u].rearrange("r p e -> r (p e)").bitcast(F32), ident_words[:])
        bias_q_ps = psum.tile([P, 2, P], F32, tag="bank2")
        words_on_all_partitions(bias_q_ps[:], b_q_cols[:].rearrange("m h c -> m (h c)"))

        grouped = {}
        codes = {}
        scales = {}
        for name in ("v", "q", "k"):
            for h in range(2):
                grouped[name, h] = keep.tile([P, HALF, PACK], BF16, name="grouped_%s%d" % (name, h), align_bytes=64)
                codes[name, h] = keep.tile([P, HALF], U32, name="codes_%s%d" % (name, h), align_bytes=64)
                scales[name, h] = keep.tile([P, HALF], U8, name="scales_%s%d" % (name, h), align_bytes=64)

        def as_runs(part):
            return part.rearrange("p (a i) t -> p a t i", i=RUN)

        def regroup_v(copy, h):
            copy(out=as_runs(grouped["v", h][:]), in_=raw_v[h][:].rearrange("p t (a i) -> p a t i", i=RUN))

        def regroup_q(copy, h):
            copy(
                out=as_runs(grouped["q", h][:]),
                in_=raw_qk[h][:].rearrange("p t (a i e) -> p e a t i", i=RUN, e=2)[:, 0],
            )

        def regroup_k(copy, h, m_cols):
            copy(
                out=grouped["k", h][:].rearrange("p (c m) t -> p m t c", c=2)[:, m_cols],
                in_=raw_qk[h][:].rearrange("p t (m c e) -> p e m t c", c=2, e=2)[:, 1, m_cols],
            )

        def quantise_w(name, h):
            quantise(codes[name, h][:], scales[name, h][:], grouped[name, h][:].rearrange("p f t -> p (f t)"))

        bias_v_rows = keep.tile([P, NE, 2], F32)
        bias_q_rows = keep.tile([P, P], F32)

        nc.gpsimd.tensor_scalar(
            out=grouped["v", 0][:],
            in0=raw_v[0][:].rearrange("p t w -> p w t"),
            scalar1=1.0,
            scalar2=0.0,
            op0=ALU.mult,
            op1=ALU.add,
        )

        regroup_v(nc.scalar.copy, 1)
        for s in range(2):
            half = slice(s * NE, (s + 1) * NE)
            nc.scalar.copy(out=bias_v_rows[half, :, :], in_=bias_v_ps[half, :, half].rearrange("r u p -> r p u"))
        nc.scalar.copy(
            out=x_grouped[:]
            .rearrange("p a m t -> p (a m t)")
            .bitcast(F32)
            .rearrange("p (a m u) -> p a m u", a=PARITIES, u=2),
            in_=x_t[:].rearrange("p u (m a) -> p a m u", a=PARITIES),
        )
        regroup_q(nc.scalar.copy, 1)
        for s in range(2):
            half = slice(s * NE, (s + 1) * NE)
            nc.scalar.copy(out=bias_q_rows[half, :], in_=bias_q_ps[half, s, :])
        regroup_k(nc.scalar.copy, 0, slice(0, P))

        acc = {}

        def product(name):
            for a in range(PARITIES):
                acc[name, a] = psum.tile([P, HALF], F32, name="acc_%s%d" % (name, a))
                for s in range(2):
                    start_col = (2 * a + 1 - s) * NE
                    window = slice(start_col, start_col + P)
                    nc.tensor.matmul_mx(
                        out=acc[name, a][:],
                        lhsT=x_codes[:, window].bitcast(FP8X4),
                        lhsT_scale=x_scales[:, window],
                        rhs=codes[name, s][:].bitcast(FP8X4),
                        rhs_scale=scales[name, s][:],
                        start=(s == 0),
                        stop=(s == 1),
                    )

        result = {}
        for name in ("v", "q"):
            result[name] = keep.tile([P, HEADS, PARITIES, HD], F32, name="%s_sb" % name)
        bias_rows = {
            "v": bias_v_rows[:].rearrange("r p u -> r (p u)").bitcast(BF16),
            "q": bias_q_rows[:].bitcast(BF16),
        }

        def add_bias(name, a):
            nc.vector.tensor_tensor(
                out=result[name][:, :, a, :],
                in0=acc[name, a][:].rearrange("r (h j) -> r h j", j=HD),
                in1=bias_rows[name].rearrange("r (h j) -> r h j", j=HD),
                op=ALU.add,
            )

        def store(name, out_dram):
            for b in range(BATCH):
                for s in range(2):
                    rows = s * NE + b * PAIRS
                    nc.sync.dma_start(
                        out=out_dram[b, s * HEADS : (s + 1) * HEADS].rearrange("h (n a) j -> n h (a j)", a=PARITIES),
                        in_=result[name][rows : rows + PAIRS, :, :, :].rearrange("n h a j -> n h (a j)"),
                    )

        k_dram = out_1.rearrange("b h j n -> b (h j) n")
        k_sb = []
        for h in range(2):
            k_sb.append(keep.tile([P, BATCH, 2, NE], F32, name="k_sb%d" % h))

        def product_k(h, c):
            acc["k", h, c] = psum.tile([P, 2 * P], F32, name="acc_k%d%d" % (h, c), tag="bank%d" % (2 * h + c))
            m_cols = slice(c * P, (c + 1) * P)
            x_cols = slice(NE, X_BLOCKS * NE)
            multiply(
                acc["k", h, c][:],
                codes["k", h][:, m_cols],
                scales["k", h][:, m_cols],
                x_codes[:, x_cols],
                x_scales[:, x_cols],
            )

        def k_in_order(h, c):
            return acc["k", h, c][:].rearrange("m (a z b n) -> m z b n a", a=PARITIES, z=2, b=BATCH)[:, 0]

        def k_place(h, c):
            return k_sb[h][:, :, c, :].rearrange("m b (n a) -> m b n a", a=PARITIES)

        def finish_k_scalar(h, c):
            nc.scalar.activation(
                out=k_place(h, c), in_=k_in_order(h, c), func=ACT.Identity, bias=bias_k[:, h, c : c + 1], scale=1.0
            )

        def finish_k_vector(h, c):
            nc.vector.tensor_scalar_add(out=k_place(h, c), in0=k_in_order(h, c), scalar1=bias_k[:, h, c : c + 1])

        def store_k(h):
            nc.sync.dma_start(
                out=k_dram[:, h * HALF : (h + 1) * HALF, :].rearrange("b (m c) n -> m b (c n)", c=2),
                in_=k_sb[h][:].rearrange("m b c n -> m b (c n)"),
            )

        quantise_w("v", 0)
        regroup_q(nc.vector.tensor_copy, 0)
        quantise_w("v", 1)
        for a in range(PARITIES):
            quantise(x_codes[:, x_block(a)], x_scales[:, x_block(a)], x_grouped[:, a, :, :].rearrange("p m t -> p (m t)"))
        product("v")
        quantise_w("q", 0)
        regroup_k(nc.vector.tensor_copy, 1, slice(0, P))
        add_bias("v", 0)
        quantise_w("q", 1)
        product("q")
        add_bias("v", 1)
        store("v", out_2)
        quantise_w("k", 1)
        product_k(1, 0)
        product_k(1, 1)
        add_bias("q", 0)
        add_bias("q", 1)
        store("q", out_0)
        quantise_w("k", 0)
        product_k(0, 0)
        product_k(0, 1)
        finish_k_scalar(1, 0)
        finish_k_scalar(1, 1)
        store_k(1)
        finish_k_scalar(0, 0)
        finish_k_vector(0, 1)
        store_k(0)
